import numpy as np
import ml_dtypes


def mxq(x, axis, fmt="e4m3"):
    dtype, down = {"e4m3": (ml_dtypes.float8_e4m3fn, 7), "e5m2": (ml_dtypes.float8_e5m2, 14)}[fmt]
    v = np.moveaxis(np.asarray(x, np.float32).astype(ml_dtypes.bfloat16).astype(np.float64), axis, -1)
    blocks = v.reshape(v.shape[:-1] + (-1, 32))
    amax = np.abs(blocks).max(-1, keepdims=True)
    byte = np.maximum(np.where(amax > 0, np.frexp(amax)[1] - 1 + 127, 0) - down, 1)
    scale = np.exp2(byte - 127.0)
    codes = (blocks / scale).astype(np.float32).astype(dtype).astype(np.float64)
    return np.moveaxis((codes * scale).reshape(v.shape), -1, axis)


WIDE = False


def mx_kscale(k):
    if not WIDE:
        return np.ones(k)
    levels = np.array([10, -10, 5, -5, 0])
    a = np.random.permutation(np.resize(levels, k // 512 * 4)).reshape(k // 512, 4)
    idx = np.arange(k)
    return np.exp2(a[idx // 512, idx % 128 // 32])


BF16 = ml_dtypes.bfloat16


def bf(x):
    return np.asarray(x, np.float32).astype(BF16)


def f64(x):
    return np.asarray(x).astype(np.float64)


E2M1 = np.array([0.0, 0.5, 1.0, 1.5, 2.0, 3.0, 4.0, 6.0, -0.0, -0.5, -1.0, -1.5, -2.0, -3.0, -4.0, -6.0])


def pack_weight(w, fmt):
    k, n = w.shape
    w = f64(bf(w)).reshape(k // 32, 32, n)
    amax = np.abs(w).max(1)
    if fmt == "e4m3":
        byte = np.frexp(amax)[1] - 1 + 127 - 7
    else:
        mant, ex = np.frexp(amax / 6.0)
        byte = np.where(mant > 0.5, ex, ex - 1) + 127
    byte = np.clip(np.where(amax > 0, byte, 1), 1, 254)
    scaled = (w * np.exp2(127.0 - byte)[:, None, :]).reshape(k, n).astype(np.float32)
    by_word = np.ascontiguousarray(scaled.reshape(k // 512, 128, 4, n).transpose(0, 1, 3, 2))
    if fmt == "e4m3":
        words = by_word.astype(ml_dtypes.float8_e4m3fn).view(np.uint8)
    else:
        c = by_word.astype(ml_dtypes.float4_e2m1fn).view(np.uint8) & 0xF
        words = c[..., 0::2] | (c[..., 1::2] << 4)
    return np.ascontiguousarray(words), np.ascontiguousarray(byte.astype(np.uint8).reshape(k // 512, 16, n))


def unpack_weight(words, scales, fmt):
    g, p, n, _ = words.shape
    if fmt == "e4m3":
        vals = np.ascontiguousarray(words).view(ml_dtypes.float8_e4m3fn).astype(np.float64)
    else:
        nib = np.empty((g, p, n, 4), np.uint8)
        nib[..., 0::2] = words & 0xF
        nib[..., 1::2] = words >> 4
        vals = E2M1[nib]
    vals = vals * np.repeat(np.exp2(scales.astype(np.float64) - 127.0), 8, axis=1)[..., None]
    return vals.transpose(0, 1, 3, 2).reshape(g * 512, n)


N, M, P, D = 4096, 1024, 1024, 16
LN_EPS = 1e-5
LENGTHSCALE = 1.0
INPUT_LB, INPUT_UB = -2.0, 2.0


def setup_inputs():
    s = mx_kscale(M)
    r = s.max() / s
    c = np.random.standard_normal(D)
    c = (c - c.mean()) / c.std()
    x = c + np.random.standard_normal((N, D)) * 1.6 / D
    z = c + np.random.uniform(INPUT_LB, INPUT_UB, (M, D)) * 1.6 / D
    z[:, 0] += np.log(r) * LENGTHSCALE
    g = np.random.standard_normal((M, P)) * 4.0 / np.sqrt(M)
    w = np.triu(g) + 0.1 * np.tril(g, -1) + np.eye(M, P)
    words, scales = pack_weight(w * r[:, None], "e4m3")
    return {"x": bf(x), "design_points": bf(z), "chol_inv_words": words, "chol_inv_scales": scales}


def reference(x, design_points, chol_inv_words, chol_inv_scales):
    x, z = f64(x), f64(design_points)
    mean = np.mean(x, axis=-1, keepdims=True)
    var = np.mean(np.square(x - mean), axis=-1, keepdims=True)
    xn = (x - mean) / np.sqrt(var + LN_EPS)
    l1 = np.zeros((N, M))
    for d in range(D):
        l1 = l1 + np.abs(xn[:, d, None] - z[None, :, d])
    kmat = np.exp(-l1 / LENGTHSCALE)
    return mxq(kmat, 1, "e4m3") @ unpack_weight(chol_inv_words, chol_inv_scales, "e4m3")

@@ -1,0 +1,285 @@
+from contextlib import ExitStack
+
+import concourse.mybir as mybir
+from concourse.masks import make_identity
+
+F32 = mybir.dt.float32
+BF16 = mybir.dt.bfloat16
+I32 = mybir.dt.int32
+U32 = mybir.dt.uint32
+U8 = mybir.dt.uint8
+FP8X4 = mybir.dt.float8_e4m3fn_x4
+ALU = mybir.AluOpType
+ACT = mybir.ActivationFunctionType
+AX = mybir.AxisListType
+
+N_ROWS = 4096
+M_POINTS = 1024
+N_OUT = 1024
+D = 16
+LN_EPS = 1e-5
+
+P = 128
+PACK = 4
+K_PASS = P * PACK
+PASSES = M_POINTS // K_PASS
+BLOCKS = PASSES * PACK
+ROW_TILES = N_ROWS // P
+BANK = 512
+OUT_BANKS = N_OUT // BANK
+
+SCALAR_DIMS = 7
+VECTOR_DIMS = D - SCALAR_DIMS
+
+FLOPS = 2 * N_ROWS * M_POINTS * N_OUT
+
+
+def tile_tmk_kernel(tc, x, design_points, chol_inv_words, chol_inv_scales, out):
+    nc = tc.nc
+    with ExitStack() as stack:
+        stack.enter_context(tc.manual_schedule())
+        const = stack.enter_context(tc.tile_pool(name="const", bufs=1))
+        work = stack.enter_context(tc.tile_pool(name="work", bufs=2))
+        psum = stack.enter_context(tc.psum_pool(name="psum", bufs=1))
+
+        z_rows = const.tile([P, PASSES, PACK, D], BF16)
+        nc.sync.dma_start(
+            out=z_rows[:],
+            in_=design_points.rearrange("(g p t) d -> p g t d", g=PASSES, p=P, t=PACK),
+        )
+        x_bf = const.tile([P, ROW_TILES, D], BF16)
+        nc.scalar.dma_start(out=x_bf[:], in_=x.rearrange("(p i) d -> p i d", i=ROW_TILES))
+
+        w_scales = const.tile([P, PASSES, N_OUT], U8, align_bytes=64)
+        nc.vector.memset(w_scales[:].bitcast(I32), 0)
+        for quadrant in range(4):
+            nc.sync.dma_start(
+                out=w_scales[32 * quadrant : 32 * quadrant + 4, :, :].bitcast(I32),
+                in_=chol_inv_scales[:, 4 * quadrant : 4 * quadrant + 4, :]
+                .rearrange("g r n -> r g n")
+                .bitcast(I32),
+            )
+        w_codes = const.tile([P, PASSES, N_OUT], U32, align_bytes=64)
+        for g in range(PASSES):
+            nc.sync.dma_start(
+                out=w_codes[:, g, :].bitcast(I32),
+                in_=chol_inv_words[g].rearrange("p n t -> p (n t)").bitcast(I32),
+            )
+
+        ident_bf = const.tile([P, P], BF16)
+        make_identity(nc, ident_bf[:])
+        ident_f32 = const.tile([P, P], F32)
+        make_identity(nc, ident_f32[:])
+
+        z_sum = const.tile([P, PASSES, PACK], F32)
+        nc.vector.reduce_sum(out=z_sum[:], in_=z_rows[:, :, :, SCALAR_DIMS:], axis=AX.X)
+        z_part_cols = const.tile([P, BLOCKS, P], F32)
+        nc.vector.tensor_scalar_mul(
+            out=z_part_cols[:],
+            in0=z_sum[:].rearrange("p g t -> p (g t)").unsqueeze(2).to_broadcast([P, BLOCKS, P]),
+            scalar1=-1.0,
+        )
+        nc.vector.tensor_scalar_mul(
+            out=z_rows[:, :, :, SCALAR_DIMS:], in0=z_rows[:, :, :, SCALAR_DIMS:], scalar1=2.0
+        )
+
+        row_sum = const.tile([P, ROW_TILES], F32)
+        nc.vector.reduce_sum(out=row_sum[:], in_=x_bf[:], axis=AX.X)
+        mean = const.tile([P, ROW_TILES], F32)
+        nc.vector.tensor_scalar_mul(out=mean[:], in0=row_sum[:], scalar1=1.0 / D)
+        centred = const.tile([P, ROW_TILES, D], F32)
+        nc.vector.tensor_tensor(
+            out=centred[:],
+            in0=x_bf[:],
+            in1=mean[:].unsqueeze(2).to_broadcast([P, ROW_TILES, D]),
+            op=ALU.subtract,
+        )
+        squares = const.tile([P, ROW_TILES, D], F32)
+        nc.vector.tensor_tensor(out=squares[:], in0=centred[:], in1=centred[:], op=ALU.mult)
+        square_sum = const.tile([P, ROW_TILES], F32)
+        nc.vector.reduce_sum(out=square_sum[:], in_=squares[:], axis=AX.X)
+        var_eps = const.tile([P, ROW_TILES], F32)
+        nc.vector.tensor_scalar(
+            out=var_eps[:], in0=square_sum[:], scalar1=1.0 / D, scalar2=LN_EPS, op0=ALU.mult, op1=ALU.add
+        )
+        std = const.tile([P, ROW_TILES], F32)
+        nc.scalar.activation(out=std[:], in_=var_eps[:], func=ACT.Sqrt)
+        rstd_rough = const.tile([P, ROW_TILES], F32)
+        nc.vector.reciprocal(out=rstd_rough[:], in_=std[:])
+        y_squared = const.tile([P, ROW_TILES], F32)
+        nc.vector.tensor_tensor(out=y_squared[:], in0=rstd_rough[:], in1=rstd_rough[:], op=ALU.mult)
+        v_y_squared = const.tile([P, ROW_TILES], F32)
+        nc.vector.tensor_tensor(out=v_y_squared[:], in0=y_squared[:], in1=var_eps[:], op=ALU.mult)
+        correction = const.tile([P, ROW_TILES], F32)
+        nc.vector.tensor_scalar(
+            out=correction[:], in0=v_y_squared[:], scalar1=-0.5, scalar2=1.5, op0=ALU.mult, op1=ALU.add
+        )
+        rstd = const.tile([P, ROW_TILES], F32)
+        nc.vector.tensor_tensor(out=rstd[:], in0=rstd_rough[:], in1=correction[:], op=ALU.mult)
+        xn = const.tile([P, ROW_TILES, D], F32)
+        nc.vector.tensor_tensor(
+            out=xn[:],
+            in0=centred[:],
+            in1=rstd[:].unsqueeze(2).to_broadcast([P, ROW_TILES, D]),
+            op=ALU.mult,
+        )
+        neg_x = const.tile([P, ROW_TILES, D], F32)
+        nc.vector.tensor_scalar_mul(out=neg_x[:], in0=xn[:], scalar1=-1.0)
+        two_x = const.tile([P, ROW_TILES, D], F32)
+        nc.vector.tensor_scalar_mul(out=two_x[:], in0=xn[:], scalar1=2.0)
+        x_part = const.tile([P, ROW_TILES], F32)
+        nc.vector.reduce_sum(out=x_part[:], in_=neg_x[:, :, SCALAR_DIMS:], axis=AX.X)
+
+        z_rep = const.tile([P, D, M_POINTS], BF16)
+        build_order = [d for pair in zip(range(SCALAR_DIMS), range(SCALAR_DIMS, D)) for d in pair]
+        build_order += list(range(2 * SCALAR_DIMS, D))
+        for d in build_order:
+            z_bank = psum.tile([P, M_POINTS], BF16, tag="setup", bufs=2)
+            for b in range(BLOCKS):
+                nc.tensor.matmul(
+                    out=z_bank[:, b * P : (b + 1) * P],
+                    lhsT=z_rows[:, b // PACK, b % PACK, d : d + 1].to_broadcast([P, P]),
+                    rhs=ident_bf[:],
+                    start=True,
+                    stop=True,
+                )
+            if d < SCALAR_DIMS:
+                nc.scalar.copy(out=z_rep[:, d, :], in_=z_bank[:])
+            else:
+                nc.vector.tensor_copy(out=z_rep[:, d, :], in_=z_bank[:])
+
+        z_part = const.tile([P, M_POINTS], F32)
+        for g in range(PASSES):
+            part_bank = psum.tile([P, PACK, P], F32, tag="setup", bufs=2)
+            for t in range(PACK):
+                nc.tensor.transpose(
+                    out=part_bank[:, t, :], in_=z_part_cols[:, g * PACK + t, :], identity=ident_f32[:]
+                )
+            nc.vector.tensor_copy(
+                out=z_part[:, g * K_PASS : (g + 1) * K_PASS],
+                in_=part_bank[:].rearrange("p t n -> p (t n)"),
+            )
+
+        out_rows = out.rearrange("(p i) c -> p i c", i=ROW_TILES)
+        dist_tiles = {}
+        l1_banks = {}
+        kmat_tiles = {}
+        kmat_codes = {}
+        kmat_scales = {}
+        out_banks = {}
+
+        def distances(i):
+            dist = work.tile([P, 1 + SCALAR_DIMS, M_POINTS], F32)
+            dist_tiles[i] = dist
+            halves = [slice(g * K_PASS, (g + 1) * K_PASS) for g in range(PASSES)]
+            for cols in halves:
+                nc.vector.tensor_scalar(
+                    out=dist[:, 0, cols],
+                    in0=z_rep[:, SCALAR_DIMS, cols],
+                    scalar1=two_x[:, i, SCALAR_DIMS : SCALAR_DIMS + 1],
+                    scalar2=x_part[:, i : i + 1],
+                    op0=ALU.max,
+                    op1=ALU.add,
+                )
+            for d in range(SCALAR_DIMS + 1, D):
+                for cols in halves:
+                    nc.vector.scalar_tensor_tensor(
+                        out=dist[:, 0, cols],
+                        in0=z_rep[:, d, cols],
+                        scalar=two_x[:, i, d : d + 1],
+                        in1=dist[:, 0, cols],
+                        op0=ALU.max,
+                        op1=ALU.add,
+                    )
+            for d in range(SCALAR_DIMS):
+                nc.scalar.activation(
+                    out=dist[:, 1 + d, :],
+                    in_=z_rep[:, d, :],
+                    func=ACT.Abs,
+                    bias=neg_x[:, i, d : d + 1],
+                    scale=1.0,
+                )
+
+        def add_up_transposed(i):
+            dist = dist_tiles[i]
+            for g in range(PASSES):
+                l1_bank = psum.tile([P, PACK, P], F32, tag="l1_%d" % g, bufs=2)
+                l1_banks[(i, g)] = l1_bank
+                for t in range(PACK):
+                    cols = slice((g * PACK + t) * P, (g * PACK + t + 1) * P)
+                    nc.tensor.matmul(
+                        out=l1_bank[:, t, :],
+                        lhsT=z_part[:, cols],
+                        rhs=ident_f32[:],
+                        is_transpose=True,
+                        start=True,
+                        stop=False,
+                    )
+                    for slot in range(1 + SCALAR_DIMS):
+                        nc.tensor.matmul(
+                            out=l1_bank[:, t, :],
+                            lhsT=dist[:, slot, cols],
+                            rhs=ident_f32[:],
+                            is_transpose=True,
+                            start=False,
+                            stop=(slot == SCALAR_DIMS),
+                        )
+
+        def exponentiate(i):
+            kmat = work.tile([P, PASSES, P, PACK], BF16, align_bytes=64)
+            kmat_tiles[i] = kmat
+            for g in range(PASSES):
+                nc.scalar.activation(
+                    out=kmat[:, g, :, :],
+                    in_=l1_banks[(i, g)][:].rearrange("p t n -> p n t"),
+                    func=ACT.Exp,
+                    scale=-1.0,
+                )
+
+        def quantise(i):
+            codes = work.tile([P, PASSES, P], U32, align_bytes=64)
+            scales = work.tile([P, PASSES, P], U8, align_bytes=64)
+            kmat_codes[i] = codes
+            kmat_scales[i] = scales
+            nc.vector.quantize_mx(
+                out=codes[:].rearrange("p g n -> p (g n)").bitcast(FP8X4),
+                scales=scales[:].rearrange("p g n -> p (g n)"),
+                in_=kmat_tiles[i][:].rearrange("p g n t -> p (g n t)"),
+            )
+
+        def multiply(i):
+            codes = kmat_codes[i]
+            scales = kmat_scales[i]
+            for h in range(OUT_BANKS):
+                cols = slice(h * BANK, (h + 1) * BANK)
+                out_bank = psum.tile([P, BANK], F32, tag="out_%d" % h)
+                out_banks[(i, h)] = out_bank
+                for g in range(PASSES):
+                    nc.tensor.matmul_mx(
+                        out=out_bank[:],
+                        lhsT=codes[:, g, :].bitcast(FP8X4),
+                        lhsT_scale=scales[:, g, :],
+                        rhs=w_codes[:, g, cols].bitcast(FP8X4),
+                        rhs_scale=w_scales[:, g, cols],
+                        start=(g == 0),
+                        stop=(g == PASSES - 1),
+                    )
+
+        def store(i):
+            result = work.tile([P, N_OUT], F32, bufs=3)
+            for h in range(OUT_BANKS):
+                nc.scalar.copy(out=result[:, h * BANK : (h + 1) * BANK], in_=out_banks[(i, h)][:])
+            nc.sync.dma_start(out=out_rows[:, i, :], in_=result[:])
+
+        for s in range(ROW_TILES + 2):
+            if s >= 2:
+                quantise(s - 2)
+                multiply(s - 2)
+            if 1 <= s <= ROW_TILES:
+                add_up_transposed(s - 1)
+            if s < ROW_TILES:
+                distances(s)
+            if 1 <= s <= ROW_TILES:
+                exponentiate(s - 1)
+            if s >= 2:
+                store(s - 2)

@@ -40,7 +40,7 @@ def tile_tmk_kernel(tc, x, design_points, chol_inv_words, chol_inv_scales, out):
         stack.enter_context(tc.manual_schedule())
         const = stack.enter_context(tc.tile_pool(name="const", bufs=1))
         work = stack.enter_context(tc.tile_pool(name="work", bufs=2))
-        psum = stack.enter_context(tc.psum_pool(name="psum", bufs=1))
+        psum = stack.enter_context(tc.psum_pool(name="psum", bufs=2))
 
         z_rows = const.tile([P, PASSES, PACK, D], BF16)
         nc.sync.dma_start(
@@ -134,7 +134,7 @@ def tile_tmk_kernel(tc, x, design_points, chol_inv_words, chol_inv_scales, out):
         build_order = [d for pair in zip(range(SCALAR_DIMS), range(SCALAR_DIMS, D)) for d in pair]
         build_order += list(range(2 * SCALAR_DIMS, D))
         for d in build_order:
-            z_bank = psum.tile([P, M_POINTS], BF16, tag="setup", bufs=2)
+            z_bank = psum.tile([P, M_POINTS], BF16, tag="out_0")
             for b in range(BLOCKS):
                 nc.tensor.matmul(
                     out=z_bank[:, b * P : (b + 1) * P],
@@ -150,7 +150,7 @@ def tile_tmk_kernel(tc, x, design_points, chol_inv_words, chol_inv_scales, out):
 
         z_part = const.tile([P, M_POINTS], F32)
         for g in range(PASSES):
-            part_bank = psum.tile([P, PACK, P], F32, tag="setup", bufs=2)
+            part_bank = psum.tile([P, PACK, P], F32, tag="out_1")
             for t in range(PACK):
                 nc.tensor.transpose(
                     out=part_bank[:, t, :], in_=z_part_cols[:, g * PACK + t, :], identity=ident_f32[:]
@@ -169,7 +169,7 @@ def tile_tmk_kernel(tc, x, design_points, chol_inv_words, chol_inv_scales, out):
         out_banks = {}
 
         def distances(i):
-            dist = work.tile([P, 1 + SCALAR_DIMS, M_POINTS], F32)
+            dist = work.tile([P, 1 + SCALAR_DIMS, M_POINTS], F32, bufs=3)
             dist_tiles[i] = dist
             halves = [slice(g * K_PASS, (g + 1) * K_PASS) for g in range(PASSES)]
             for cols in halves:
@@ -203,7 +203,7 @@ def tile_tmk_kernel(tc, x, design_points, chol_inv_words, chol_inv_scales, out):
         def add_up_transposed(i):
             dist = dist_tiles[i]
             for g in range(PASSES):
-                l1_bank = psum.tile([P, PACK, P], F32, tag="l1_%d" % g, bufs=2)
+                l1_bank = psum.tile([P, PACK, P], F32, tag="l1_%d" % g)
                 l1_banks[(i, g)] = l1_bank
                 for t in range(PACK):
                     cols = slice((g * PACK + t) * P, (g * PACK + t + 1) * P)
@@ -271,15 +271,8 @@ def tile_tmk_kernel(tc, x, design_points, chol_inv_words, chol_inv_scales, out):
                 nc.scalar.copy(out=result[:, h * BANK : (h + 1) * BANK], in_=out_banks[(i, h)][:])
             nc.sync.dma_start(out=out_rows[:, i, :], in_=result[:])
 
-        for s in range(ROW_TILES + 2):
-            if s >= 2:
-                quantise(s - 2)
-                multiply(s - 2)
-            if 1 <= s <= ROW_TILES:
-                add_up_transposed(s - 1)
-            if s < ROW_TILES:
-                distances(s)
-            if 1 <= s <= ROW_TILES:
-                exponentiate(s - 1)
-            if s >= 2:
-                store(s - 2)
+        stages = [distances, add_up_transposed, exponentiate, quantise, multiply, store]
+        for s in range(ROW_TILES + len(stages) - 1):
+            for lag in reversed(range(len(stages))):
+                if 0 <= s - lag < ROW_TILES:
+                    stages[lag](s - lag)

@@ -30,6 +30,10 @@ OUT_BANKS = N_OUT // BANK
 
 SCALAR_DIMS = 7
 VECTOR_DIMS = D - SCALAR_DIMS
+CHAINS = 3
+LINKS = VECTOR_DIMS // CHAINS
+assert CHAINS * LINKS == VECTOR_DIMS
+SLOTS = CHAINS + SCALAR_DIMS
 
 FLOPS = 2 * N_ROWS * M_POINTS * N_OUT
 
@@ -127,8 +131,12 @@ def tile_tmk_kernel(tc, x, design_points, chol_inv_words, chol_inv_scales, out):
         nc.vector.tensor_scalar_mul(out=neg_x[:], in0=xn[:], scalar1=-1.0)
         two_x = const.tile([P, ROW_TILES, D], F32)
         nc.vector.tensor_scalar_mul(out=two_x[:], in0=xn[:], scalar1=2.0)
-        x_part = const.tile([P, ROW_TILES], F32)
-        nc.vector.reduce_sum(out=x_part[:], in_=neg_x[:, :, SCALAR_DIMS:], axis=AX.X)
+        x_part = const.tile([P, ROW_TILES, CHAINS], F32)
+        nc.vector.reduce_sum(
+            out=x_part[:],
+            in_=neg_x[:, :, SCALAR_DIMS:].rearrange("p i (k c) -> p i c k", c=CHAINS),
+            axis=AX.X,
+        )
 
         z_rep = const.tile([P, D, M_POINTS], BF16)
         build_order = [d for pair in zip(range(SCALAR_DIMS), range(SCALAR_DIMS, D)) for d in pair]
@@ -169,31 +177,32 @@ def tile_tmk_kernel(tc, x, design_points, chol_inv_words, chol_inv_scales, out):
         out_banks = {}
 
         def distances(i):
-            dist = work.tile([P, 1 + SCALAR_DIMS, M_POINTS], F32, bufs=3)
+            dist = work.tile([P, SLOTS, M_POINTS], F32, bufs=3)
             dist_tiles[i] = dist
-            halves = [slice(g * K_PASS, (g + 1) * K_PASS) for g in range(PASSES)]
-            for cols in halves:
-                nc.vector.tensor_scalar(
-                    out=dist[:, 0, cols],
-                    in0=z_rep[:, SCALAR_DIMS, cols],
-                    scalar1=two_x[:, i, SCALAR_DIMS : SCALAR_DIMS + 1],
-                    scalar2=x_part[:, i : i + 1],
-                    op0=ALU.max,
-                    op1=ALU.add,
-                )
-            for d in range(SCALAR_DIMS + 1, D):
-                for cols in halves:
-                    nc.vector.scalar_tensor_tensor(
-                        out=dist[:, 0, cols],
-                        in0=z_rep[:, d, cols],
-                        scalar=two_x[:, i, d : d + 1],
-                        in1=dist[:, 0, cols],
-                        op0=ALU.max,
-                        op1=ALU.add,
-                    )
+            for k in range(LINKS):
+                for c in range(CHAINS):
+                    d = SCALAR_DIMS + k * CHAINS + c
+                    if k == 0:
+                        nc.vector.tensor_scalar(
+                            out=dist[:, c, :],
+                            in0=z_rep[:, d, :],
+                            scalar1=two_x[:, i, d : d + 1],
+                            scalar2=x_part[:, i, c : c + 1],
+                            op0=ALU.max,
+                            op1=ALU.add,
+                        )
+                    else:
+                        nc.vector.scalar_tensor_tensor(
+                            out=dist[:, c, :],
+                            in0=z_rep[:, d, :],
+                            scalar=two_x[:, i, d : d + 1],
+                            in1=dist[:, c, :],
+                            op0=ALU.max,
+                            op1=ALU.add,
+                        )
             for d in range(SCALAR_DIMS):
                 nc.scalar.activation(
-                    out=dist[:, 1 + d, :],
+                    out=dist[:, CHAINS + d, :],
                     in_=z_rep[:, d, :],
                     func=ACT.Abs,
                     bias=neg_x[:, i, d : d + 1],
@@ -205,24 +214,17 @@ def tile_tmk_kernel(tc, x, design_points, chol_inv_words, chol_inv_scales, out):
             for g in range(PASSES):
                 l1_bank = psum.tile([P, PACK, P], F32, tag="l1_%d" % g)
                 l1_banks[(i, g)] = l1_bank
-                for t in range(PACK):
-                    cols = slice((g * PACK + t) * P, (g * PACK + t + 1) * P)
-                    nc.tensor.matmul(
-                        out=l1_bank[:, t, :],
-                        lhsT=z_part[:, cols],
-                        rhs=ident_f32[:],
-                        is_transpose=True,
-                        start=True,
-                        stop=False,
-                    )
-                    for slot in range(1 + SCALAR_DIMS):
+            for t in range(PACK):
+                for slot in range(-1, SLOTS):
+                    for g in range(PASSES):
+                        cols = slice((g * PACK + t) * P, (g * PACK + t + 1) * P)
                         nc.tensor.matmul(
-                            out=l1_bank[:, t, :],
-                            lhsT=dist[:, slot, cols],
+                            out=l1_banks[(i, g)][:, t, :],
+                            lhsT=z_part[:, cols] if slot < 0 else dist[:, slot, cols],
                             rhs=ident_f32[:],
                             is_transpose=True,
-                            start=False,
-                            stop=(slot == SCALAR_DIMS),
+                            start=(slot < 0),
+                            stop=(slot == SLOTS - 1),
                         )
 
         def exponentiate(i):
@@ -267,8 +269,8 @@ def tile_tmk_kernel(tc, x, design_points, chol_inv_words, chol_inv_scales, out):
 
         def store(i):
             result = work.tile([P, N_OUT], F32, bufs=3)
-            for h in range(OUT_BANKS):
-                nc.scalar.copy(out=result[:, h * BANK : (h + 1) * BANK], in_=out_banks[(i, h)][:])
+            nc.scalar.copy(out=result[:, :BANK], in_=out_banks[(i, 0)][:])
+            nc.vector.tensor_copy(out=result[:, BANK:], in_=out_banks[(i, 1)][:])
             nc.sync.dma_start(out=out_rows[:, i, :], in_=result[:])
 
         stages = [distances, add_up_transposed, exponentiate, quantise, multiply, store]

@@ -209,12 +209,13 @@ def tile_tmk_kernel(tc, x, design_points, chol_inv_words, chol_inv_scales, out):
                     scale=1.0,
                 )
 
-        def add_up_transposed(i):
+        def add_up_transposed(i, half):
             dist = dist_tiles[i]
-            for g in range(PASSES):
-                l1_bank = psum.tile([P, PACK, P], F32, tag="l1_%d" % g)
-                l1_banks[(i, g)] = l1_bank
-            for t in range(PACK):
+            if half == 0:
+                for g in range(PASSES):
+                    l1_bank = psum.tile([P, PACK, P], F32, tag="l1_%d" % g)
+                    l1_banks[(i, g)] = l1_bank
+            for t in range(half * PACK // 2, (half + 1) * PACK // 2):
                 for slot in range(-1, SLOTS):
                     for g in range(PASSES):
                         cols = slice((g * PACK + t) * P, (g * PACK + t + 1) * P)
@@ -249,23 +250,20 @@ def tile_tmk_kernel(tc, x, design_points, chol_inv_words, chol_inv_scales, out):
                 in_=kmat_tiles[i][:].rearrange("p g n t -> p (g n t)"),
             )
 
-        def multiply(i):
-            codes = kmat_codes[i]
-            scales = kmat_scales[i]
-            for h in range(OUT_BANKS):
-                cols = slice(h * BANK, (h + 1) * BANK)
-                out_bank = psum.tile([P, BANK], F32, tag="out_%d" % h)
-                out_banks[(i, h)] = out_bank
-                for g in range(PASSES):
-                    nc.tensor.matmul_mx(
-                        out=out_bank[:],
-                        lhsT=codes[:, g, :].bitcast(FP8X4),
-                        lhsT_scale=scales[:, g, :],
-                        rhs=w_codes[:, g, cols].bitcast(FP8X4),
-                        rhs_scale=w_scales[:, g, cols],
-                        start=(g == 0),
-                        stop=(g == PASSES - 1),
-                    )
+        def multiply(i, h):
+            cols = slice(h * BANK, (h + 1) * BANK)
+            out_bank = psum.tile([P, BANK], F32, tag="out_%d" % h)
+            out_banks[(i, h)] = out_bank
+            for g in range(PASSES):
+                nc.tensor.matmul_mx(
+                    out=out_bank[:],
+                    lhsT=kmat_codes[i][:, g, :].bitcast(FP8X4),
+                    lhsT_scale=kmat_scales[i][:, g, :],
+                    rhs=w_codes[:, g, cols].bitcast(FP8X4),
+                    rhs_scale=w_scales[:, g, cols],
+                    start=(g == 0),
+                    stop=(g == PASSES - 1),
+                )
 
         def store(i):
             result = work.tile([P, N_OUT], F32, bufs=3)
@@ -273,8 +271,20 @@ def tile_tmk_kernel(tc, x, design_points, chol_inv_words, chol_inv_scales, out):
             nc.vector.tensor_copy(out=result[:, BANK:], in_=out_banks[(i, 1)][:])
             nc.sync.dma_start(out=out_rows[:, i, :], in_=result[:])
 
-        stages = [distances, add_up_transposed, exponentiate, quantise, multiply, store]
-        for s in range(ROW_TILES + len(stages) - 1):
-            for lag in reversed(range(len(stages))):
-                if 0 <= s - lag < ROW_TILES:
-                    stages[lag](s - lag)
+        def live(i):
+            return 0 <= i < ROW_TILES
+
+        for s in range(ROW_TILES + 5):
+            if live(s - 5):
+                store(s - 5)
+            for half in range(2):
+                if live(s - 4):
+                    multiply(s - 4, half)
+                if live(s - 1):
+                    add_up_transposed(s - 1, half)
+            if live(s - 3):
+                quantise(s - 3)
+            if live(s - 2):
+                exponentiate(s - 2)
+            if live(s):
+                distances(s)

@@ -28,11 +28,11 @@ ROW_TILES = N_ROWS // P
 BANK = 512
 OUT_BANKS = N_OUT // BANK
 
-SCALAR_DIMS = 7
+SCALAR_DIMS = 6
 VECTOR_DIMS = D - SCALAR_DIMS
-CHAINS = 3
+CHAINS = 4
 LINKS = VECTOR_DIMS // CHAINS
-assert CHAINS * LINKS == VECTOR_DIMS
+EXTRA = VECTOR_DIMS - CHAINS * LINKS
 SLOTS = CHAINS + SCALAR_DIMS
 
 FLOPS = 2 * N_ROWS * M_POINTS * N_OUT
@@ -134,8 +134,11 @@ def tile_tmk_kernel(tc, x, design_points, chol_inv_words, chol_inv_scales, out):
         x_part = const.tile([P, ROW_TILES, CHAINS], F32)
         nc.vector.reduce_sum(
             out=x_part[:],
-            in_=neg_x[:, :, SCALAR_DIMS:].rearrange("p i (k c) -> p i c k", c=CHAINS),
+            in_=neg_x[:, :, SCALAR_DIMS : D - EXTRA].rearrange("p i (k c) -> p i c k", c=CHAINS),
             axis=AX.X,
+        )
+        nc.vector.tensor_tensor(
+            out=x_part[:, :, :EXTRA], in0=x_part[:, :, :EXTRA], in1=neg_x[:, :, D - EXTRA :], op=ALU.add
         )
 
         z_rep = const.tile([P, D, M_POINTS], BF16)
@@ -179,8 +182,8 @@ def tile_tmk_kernel(tc, x, design_points, chol_inv_words, chol_inv_scales, out):
         def distances(i):
             dist = work.tile([P, SLOTS, M_POINTS], F32, bufs=3)
             dist_tiles[i] = dist
-            for k in range(LINKS):
-                for c in range(CHAINS):
+            for k in range(LINKS + 1):
+                for c in range(CHAINS if k < LINKS else EXTRA):
                     d = SCALAR_DIMS + k * CHAINS + c
                     if k == 0:
                         nc.vector.tensor_scalar(
@@ -268,7 +271,7 @@ def tile_tmk_kernel(tc, x, design_points, chol_inv_words, chol_inv_scales, out):
         def store(i):
             result = work.tile([P, N_OUT], F32, bufs=3)
             nc.scalar.copy(out=result[:, :BANK], in_=out_banks[(i, 0)][:])
-            nc.vector.tensor_copy(out=result[:, BANK:], in_=out_banks[(i, 1)][:])
+            nc.scalar.copy(out=result[:, BANK:], in_=out_banks[(i, 1)][:])
             nc.sync.dma_start(out=out_rows[:, i, :], in_=result[:])
 
         def live(i):

@@ -35,6 +35,8 @@ LINKS = VECTOR_DIMS // CHAINS
 EXTRA = VECTOR_DIMS - CHAINS * LINKS
 SLOTS = CHAINS + SCALAR_DIMS
 
+EARLY = 2
+
 FLOPS = 2 * N_ROWS * M_POINTS * N_OUT
 
 
@@ -75,28 +77,49 @@ def tile_tmk_kernel(tc, x, design_points, chol_inv_words, chol_inv_scales, out):
         ident_f32 = const.tile([P, P], F32)
         make_identity(nc, ident_f32[:])
 
-        z_sum = const.tile([P, PASSES, PACK], F32)
-        nc.vector.reduce_sum(out=z_sum[:], in_=z_rows[:, :, :, SCALAR_DIMS:], axis=AX.X)
-        z_part_cols = const.tile([P, BLOCKS, P], F32)
-        nc.vector.tensor_scalar_mul(
-            out=z_part_cols[:],
-            in0=z_sum[:].rearrange("p g t -> p (g t)").unsqueeze(2).to_broadcast([P, BLOCKS, P]),
-            scalar1=-1.0,
+        one = const.tile([P, 1], F32)
+        nc.vector.memset(one[:], 1.0)
+        warm = const.tile([P, 1], F32)
+        nc.scalar.activation(out=warm[:], in_=one[:], func=ACT.Sqrt)
+
+        z_sum = const.tile([P, BLOCKS], F32)
+        nc.vector.reduce_sum(
+            out=z_sum[:], in_=z_rows[:, :, :, SCALAR_DIMS:].rearrange("p g t d -> p (g t) d"), axis=AX.X
         )
+        neg_z_sum = const.tile([P, BLOCKS], F32)
+        nc.vector.tensor_scalar_mul(out=neg_z_sum[:], in0=z_sum[:], scalar1=-1.0)
         nc.vector.tensor_scalar_mul(
             out=z_rows[:, :, :, SCALAR_DIMS:], in0=z_rows[:, :, :, SCALAR_DIMS:], scalar1=2.0
         )
 
+        z_rep = const.tile([P, D, M_POINTS], BF16)
+        bank_tags = ["l1_0", "l1_1", "out_0", "out_1"]
+
+        def repeat_z(d):
+            z_bank = psum.tile([P, M_POINTS], BF16, tag=bank_tags[d % len(bank_tags)])
+            for b in range(BLOCKS):
+                nc.tensor.matmul(
+                    out=z_bank[:, b * P : (b + 1) * P],
+                    lhsT=z_rows[:, b // PACK, b % PACK, d : d + 1].to_broadcast([P, P]),
+                    rhs=ident_bf[:],
+                    start=True,
+                    stop=True,
+                )
+            nc.scalar.copy(out=z_rep[:, d, :], in_=z_bank[:])
+
+        for d in range(SCALAR_DIMS, SCALAR_DIMS + EARLY):
+            repeat_z(d)
+
         row_sum = const.tile([P, ROW_TILES], F32)
         nc.vector.reduce_sum(out=row_sum[:], in_=x_bf[:], axis=AX.X)
-        mean = const.tile([P, ROW_TILES], F32)
-        nc.vector.tensor_scalar_mul(out=mean[:], in0=row_sum[:], scalar1=1.0 / D)
         centred = const.tile([P, ROW_TILES, D], F32)
-        nc.vector.tensor_tensor(
+        nc.vector.scalar_tensor_tensor(
             out=centred[:],
             in0=x_bf[:],
-            in1=mean[:].unsqueeze(2).to_broadcast([P, ROW_TILES, D]),
-            op=ALU.subtract,
+            scalar=float(D),
+            in1=row_sum[:].unsqueeze(2).to_broadcast([P, ROW_TILES, D]),
+            op0=ALU.mult,
+            op1=ALU.subtract,
         )
         squares = const.tile([P, ROW_TILES, D], F32)
         nc.vector.tensor_tensor(out=squares[:], in0=centred[:], in1=centred[:], op=ALU.mult)
@@ -104,7 +127,7 @@ def tile_tmk_kernel(tc, x, design_points, chol_inv_words, chol_inv_scales, out):
         nc.vector.reduce_sum(out=square_sum[:], in_=squares[:], axis=AX.X)
         var_eps = const.tile([P, ROW_TILES], F32)
         nc.vector.tensor_scalar(
-            out=var_eps[:], in0=square_sum[:], scalar1=1.0 / D, scalar2=LN_EPS, op0=ALU.mult, op1=ALU.add
+            out=var_eps[:], in0=square_sum[:], scalar1=1.0 / D**3, scalar2=LN_EPS, op0=ALU.mult, op1=ALU.add
         )
         std = const.tile([P, ROW_TILES], F32)
         nc.scalar.activation(out=std[:], in_=var_eps[:], func=ACT.Sqrt)
@@ -120,17 +143,17 @@ def tile_tmk_kernel(tc, x, design_points, chol_inv_words, chol_inv_scales, out):
         )
         rstd = const.tile([P, ROW_TILES], F32)
         nc.vector.tensor_tensor(out=rstd[:], in0=rstd_rough[:], in1=correction[:], op=ALU.mult)
-        xn = const.tile([P, ROW_TILES, D], F32)
-        nc.vector.tensor_tensor(
-            out=xn[:],
-            in0=centred[:],
-            in1=rstd[:].unsqueeze(2).to_broadcast([P, ROW_TILES, D]),
-            op=ALU.mult,
-        )
         neg_x = const.tile([P, ROW_TILES, D], F32)
-        nc.vector.tensor_scalar_mul(out=neg_x[:], in0=xn[:], scalar1=-1.0)
         two_x = const.tile([P, ROW_TILES, D], F32)
-        nc.vector.tensor_scalar_mul(out=two_x[:], in0=xn[:], scalar1=2.0)
+        for scaled, factor in ((neg_x, -1.0 / D), (two_x, 2.0 / D)):
+            nc.vector.scalar_tensor_tensor(
+                out=scaled[:],
+                in0=centred[:],
+                scalar=factor,
+                in1=rstd[:].unsqueeze(2).to_broadcast([P, ROW_TILES, D]),
+                op0=ALU.mult,
+                op1=ALU.mult,
+            )
         x_part = const.tile([P, ROW_TILES, CHAINS], F32)
         nc.vector.reduce_sum(
             out=x_part[:],
@@ -141,36 +164,6 @@ def tile_tmk_kernel(tc, x, design_points, chol_inv_words, chol_inv_scales, out):
             out=x_part[:, :, :EXTRA], in0=x_part[:, :, :EXTRA], in1=neg_x[:, :, D - EXTRA :], op=ALU.add
         )
 
-        z_rep = const.tile([P, D, M_POINTS], BF16)
-        build_order = [d for pair in zip(range(SCALAR_DIMS), range(SCALAR_DIMS, D)) for d in pair]
-        build_order += list(range(2 * SCALAR_DIMS, D))
-        for d in build_order:
-            z_bank = psum.tile([P, M_POINTS], BF16, tag="out_0")
-            for b in range(BLOCKS):
-                nc.tensor.matmul(
-                    out=z_bank[:, b * P : (b + 1) * P],
-                    lhsT=z_rows[:, b // PACK, b % PACK, d : d + 1].to_broadcast([P, P]),
-                    rhs=ident_bf[:],
-                    start=True,
-                    stop=True,
-                )
-            if d < SCALAR_DIMS:
-                nc.scalar.copy(out=z_rep[:, d, :], in_=z_bank[:])
-            else:
-                nc.vector.tensor_copy(out=z_rep[:, d, :], in_=z_bank[:])
-
-        z_part = const.tile([P, M_POINTS], F32)
-        for g in range(PASSES):
-            part_bank = psum.tile([P, PACK, P], F32, tag="out_1")
-            for t in range(PACK):
-                nc.tensor.transpose(
-                    out=part_bank[:, t, :], in_=z_part_cols[:, g * PACK + t, :], identity=ident_f32[:]
-                )
-            nc.vector.tensor_copy(
-                out=z_part[:, g * K_PASS : (g + 1) * K_PASS],
-                in_=part_bank[:].rearrange("p t n -> p (t n)"),
-            )
-
         out_rows = out.rearrange("(p i) c -> p i c", i=ROW_TILES)
         dist_tiles = {}
         l1_banks = {}
@@ -179,9 +172,12 @@ def tile_tmk_kernel(tc, x, design_points, chol_inv_words, chol_inv_scales, out):
         kmat_scales = {}
         out_banks = {}
 
-        def distances(i):
+        def new_dist(i):
             dist = work.tile([P, SLOTS, M_POINTS], F32, bufs=3)
             dist_tiles[i] = dist
+
+        def vector_distances(i):
+            dist = dist_tiles[i]
             for k in range(LINKS + 1):
                 for c in range(CHAINS if k < LINKS else EXTRA):
                     d = SCALAR_DIMS + k * CHAINS + c
@@ -203,14 +199,15 @@ def tile_tmk_kernel(tc, x, design_points, chol_inv_words, chol_inv_scales, out):
                             op0=ALU.max,
                             op1=ALU.add,
                         )
-            for d in range(SCALAR_DIMS):
-                nc.scalar.activation(
-                    out=dist[:, CHAINS + d, :],
-                    in_=z_rep[:, d, :],
-                    func=ACT.Abs,
-                    bias=neg_x[:, i, d : d + 1],
-                    scale=1.0,
-                )
+
+        def scalar_distance(i, d):
+            nc.scalar.activation(
+                out=dist_tiles[i][:, CHAINS + d, :],
+                in_=z_rep[:, d, :],
+                func=ACT.Abs,
+                bias=neg_x[:, i, d : d + 1],
+                scale=1.0,
+            )
 
         def add_up_transposed(i, half):
             dist = dist_tiles[i]
@@ -274,10 +271,32 @@ def tile_tmk_kernel(tc, x, design_points, chol_inv_words, chol_inv_scales, out):
             nc.scalar.copy(out=result[:, BANK:], in_=out_banks[(i, 1)][:])
             nc.sync.dma_start(out=out_rows[:, i, :], in_=result[:])
 
+        for d in range(SCALAR_DIMS + EARLY, D):
+            repeat_z(d)
+        z_part = const.tile([P, M_POINTS], F32)
+        for g in range(PASSES):
+            part_bank = psum.tile([P, PACK, P], F32, tag=bank_tags[g])
+            for t in range(PACK):
+                b = g * PACK + t
+                nc.tensor.transpose(
+                    out=part_bank[:, t, :], in_=neg_z_sum[:, b : b + 1].to_broadcast([P, P]), identity=ident_f32[:]
+                )
+            nc.scalar.copy(
+                out=z_part[:, g * K_PASS : (g + 1) * K_PASS],
+                in_=part_bank[:].rearrange("p t n -> p (t n)"),
+            )
+        new_dist(0)
+        vector_distances(0)
+        repeat_z(0)
+        for d in range(SCALAR_DIMS):
+            if d + 1 < SCALAR_DIMS:
+                repeat_z(d + 1)
+            scalar_distance(0, d)
+
         def live(i):
             return 0 <= i < ROW_TILES
 
-        for s in range(ROW_TILES + 5):
+        for s in range(1, ROW_TILES + 5):
             if live(s - 5):
                 store(s - 5)
             for half in range(2):
@@ -290,4 +309,7 @@ def tile_tmk_kernel(tc, x, design_points, chol_inv_words, chol_inv_scales, out):
             if live(s - 2):
                 exponentiate(s - 2)
             if live(s):
-                distances(s)
+                new_dist(s)
+                vector_distances(s)
+                for d in range(SCALAR_DIMS):
+                    scalar_distance(s, d)

@@ -299,10 +299,11 @@ def tile_tmk_kernel(tc, x, design_points, chol_inv_words, chol_inv_scales, out):
         for s in range(1, ROW_TILES + 5):
             if live(s - 5):
                 store(s - 5)
-            for half in range(2):
-                if live(s - 4):
-                    multiply(s - 4, half)
-                if live(s - 1):
+            if live(s - 4):
+                for h in range(OUT_BANKS):
+                    multiply(s - 4, h)
+            if live(s - 1):
+                for half in range(2):
                     add_up_transposed(s - 1, half)
             if live(s - 3):
                 quantise(s - 3)

@@ -30,10 +30,9 @@ OUT_BANKS = N_OUT // BANK
 
 SCALAR_DIMS = 6
 VECTOR_DIMS = D - SCALAR_DIMS
-CHAINS = 4
-LINKS = VECTOR_DIMS // CHAINS
-EXTRA = VECTOR_DIMS - CHAINS * LINKS
-SLOTS = CHAINS + SCALAR_DIMS
+CHAIN_COUNTS = (4, 5)
+MAX_CHAINS = max(CHAIN_COUNTS)
+SLOTS = MAX_CHAINS + SCALAR_DIMS
 
 EARLY = 2
 
@@ -154,15 +153,20 @@ def tile_tmk_kernel(tc, x, design_points, chol_inv_words, chol_inv_scales, out):
                 op0=ALU.mult,
                 op1=ALU.mult,
             )
-        x_part = const.tile([P, ROW_TILES, CHAINS], F32)
-        nc.vector.reduce_sum(
-            out=x_part[:],
-            in_=neg_x[:, :, SCALAR_DIMS : D - EXTRA].rearrange("p i (k c) -> p i c k", c=CHAINS),
-            axis=AX.X,
-        )
-        nc.vector.tensor_tensor(
-            out=x_part[:, :, :EXTRA], in0=x_part[:, :, :EXTRA], in1=neg_x[:, :, D - EXTRA :], op=ALU.add
-        )
+        x_parts = {}
+        for chains in CHAIN_COUNTS:
+            extra = VECTOR_DIMS % chains
+            x_part = const.tile([P, ROW_TILES, chains], F32, tag="x_part_%d" % chains)
+            x_parts[chains] = x_part
+            nc.vector.reduce_sum(
+                out=x_part[:],
+                in_=neg_x[:, :, SCALAR_DIMS : D - extra].rearrange("p i (k c) -> p i c k", c=chains),
+                axis=AX.X,
+            )
+            if extra:
+                nc.vector.tensor_tensor(
+                    out=x_part[:, :, :extra], in0=x_part[:, :, :extra], in1=neg_x[:, :, D - extra :], op=ALU.add
+                )
 
         out_rows = out.rearrange("(p i) c -> p i c", i=ROW_TILES)
         dist_tiles = {}
@@ -176,33 +180,36 @@ def tile_tmk_kernel(tc, x, design_points, chol_inv_words, chol_inv_scales, out):
             dist = work.tile([P, SLOTS, M_POINTS], F32, bufs=3)
             dist_tiles[i] = dist
 
+        def chains_of(i):
+            return CHAIN_COUNTS[i % len(CHAIN_COUNTS)]
+
         def vector_distances(i):
             dist = dist_tiles[i]
-            for k in range(LINKS + 1):
-                for c in range(CHAINS if k < LINKS else EXTRA):
-                    d = SCALAR_DIMS + k * CHAINS + c
-                    if k == 0:
-                        nc.vector.tensor_scalar(
-                            out=dist[:, c, :],
-                            in0=z_rep[:, d, :],
-                            scalar1=two_x[:, i, d : d + 1],
-                            scalar2=x_part[:, i, c : c + 1],
-                            op0=ALU.max,
-                            op1=ALU.add,
-                        )
-                    else:
-                        nc.vector.scalar_tensor_tensor(
-                            out=dist[:, c, :],
-                            in0=z_rep[:, d, :],
-                            scalar=two_x[:, i, d : d + 1],
-                            in1=dist[:, c, :],
-                            op0=ALU.max,
-                            op1=ALU.add,
-                        )
+            chains = chains_of(i)
+            for d in range(SCALAR_DIMS, D):
+                c = (d - SCALAR_DIMS) % chains
+                if d < SCALAR_DIMS + chains:
+                    nc.vector.tensor_scalar(
+                        out=dist[:, c, :],
+                        in0=z_rep[:, d, :],
+                        scalar1=two_x[:, i, d : d + 1],
+                        scalar2=x_parts[chains][:, i, c : c + 1],
+                        op0=ALU.max,
+                        op1=ALU.add,
+                    )
+                else:
+                    nc.vector.scalar_tensor_tensor(
+                        out=dist[:, c, :],
+                        in0=z_rep[:, d, :],
+                        scalar=two_x[:, i, d : d + 1],
+                        in1=dist[:, c, :],
+                        op0=ALU.max,
+                        op1=ALU.add,
+                    )
 
         def scalar_distance(i, d):
             nc.scalar.activation(
-                out=dist_tiles[i][:, CHAINS + d, :],
+                out=dist_tiles[i][:, MAX_CHAINS + d, :],
                 in_=z_rep[:, d, :],
                 func=ACT.Abs,
                 bias=neg_x[:, i, d : d + 1],
@@ -211,12 +218,13 @@ def tile_tmk_kernel(tc, x, design_points, chol_inv_words, chol_inv_scales, out):
 
         def add_up_transposed(i, half):
             dist = dist_tiles[i]
+            slots = [-1] + list(range(chains_of(i))) + list(range(MAX_CHAINS, SLOTS))
             if half == 0:
                 for g in range(PASSES):
                     l1_bank = psum.tile([P, PACK, P], F32, tag="l1_%d" % g)
                     l1_banks[(i, g)] = l1_bank
             for t in range(half * PACK // 2, (half + 1) * PACK // 2):
-                for slot in range(-1, SLOTS):
+                for slot in slots:
                     for g in range(PASSES):
                         cols = slice((g * PACK + t) * P, (g * PACK + t + 1) * P)
                         nc.tensor.matmul(
@@ -225,7 +233,7 @@ def tile_tmk_kernel(tc, x, design_points, chol_inv_words, chol_inv_scales, out):
                             rhs=ident_f32[:],
                             is_transpose=True,
                             start=(slot < 0),
-                            stop=(slot == SLOTS - 1),
+                            stop=(slot == slots[-1]),
                         )
 
         def exponentiate(i):

@@ -175,6 +175,7 @@ def tile_tmk_kernel(tc, x, design_points, chol_inv_words, chol_inv_scales, out):
         kmat_codes = {}
         kmat_scales = {}
         out_banks = {}
+        results = {}
 
         def new_dist(i):
             dist = work.tile([P, SLOTS, M_POINTS], F32, bufs=3)
@@ -216,68 +217,82 @@ def tile_tmk_kernel(tc, x, design_points, chol_inv_words, chol_inv_scales, out):
                 scale=1.0,
             )
 
-        def add_up_transposed(i, half):
-            dist = dist_tiles[i]
-            slots = [-1] + list(range(chains_of(i))) + list(range(MAX_CHAINS, SLOTS))
-            if half == 0:
-                for g in range(PASSES):
-                    l1_bank = psum.tile([P, PACK, P], F32, tag="l1_%d" % g)
-                    l1_banks[(i, g)] = l1_bank
-            for t in range(half * PACK // 2, (half + 1) * PACK // 2):
-                for slot in slots:
-                    for g in range(PASSES):
-                        cols = slice((g * PACK + t) * P, (g * PACK + t + 1) * P)
-                        nc.tensor.matmul(
-                            out=l1_banks[(i, g)][:, t, :],
-                            lhsT=z_part[:, cols] if slot < 0 else dist[:, slot, cols],
-                            rhs=ident_f32[:],
-                            is_transpose=True,
-                            start=(slot < 0),
-                            stop=(slot == slots[-1]),
-                        )
-
-        def exponentiate(i):
-            kmat = work.tile([P, PASSES, P, PACK], BF16, align_bytes=64)
-            kmat_tiles[i] = kmat
+        def open_banks(i):
             for g in range(PASSES):
-                nc.scalar.activation(
-                    out=kmat[:, g, :, :],
-                    in_=l1_banks[(i, g)][:].rearrange("p t n -> p n t"),
-                    func=ACT.Exp,
-                    scale=-1.0,
-                )
+                l1_bank = psum.tile([P, PACK, P], F32, tag="l1_%d" % g)
+                l1_banks[(i, g)] = l1_bank
 
-        def quantise(i):
-            codes = work.tile([P, PASSES, P], U32, align_bytes=64)
-            scales = work.tile([P, PASSES, P], U8, align_bytes=64)
-            kmat_codes[i] = codes
-            kmat_scales[i] = scales
-            nc.vector.quantize_mx(
-                out=codes[:].rearrange("p g n -> p (g n)").bitcast(FP8X4),
-                scales=scales[:].rearrange("p g n -> p (g n)"),
-                in_=kmat_tiles[i][:].rearrange("p g n t -> p (g n t)"),
+        def add_up_transposed(i, blocks, slots):
+            dist = dist_tiles[i]
+            for slot in slots:
+                for g, t in blocks:
+                    cols = slice((g * PACK + t) * P, (g * PACK + t + 1) * P)
+                    nc.tensor.matmul(
+                        out=l1_banks[(i, g)][:, t, :],
+                        lhsT=z_part[:, cols] if slot < 0 else dist[:, slot, cols],
+                        rhs=ident_f32[:],
+                        is_transpose=True,
+                        start=(slot == slots[0]),
+                        stop=(slot == slots[-1]),
+                    )
+
+        def all_slots(i):
+            return [-1] + list(range(chains_of(i))) + list(range(MAX_CHAINS, SLOTS))
+
+        def exponentiate(i, g):
+            if g == 0:
+                kmat = work.tile([P, PASSES, P, PACK], BF16, align_bytes=64)
+                kmat_tiles[i] = kmat
+            nc.scalar.activation(
+                out=kmat_tiles[i][:, g, :, :],
+                in_=l1_banks[(i, g)][:].rearrange("p t n -> p n t"),
+                func=ACT.Exp,
+                scale=-1.0,
             )
 
-        def multiply(i, h):
+        def quantise(i, first, count):
+            if first == 0:
+                codes = work.tile([P, PASSES, P], U32, align_bytes=64)
+                scales = work.tile([P, PASSES, P], U8, align_bytes=64)
+                kmat_codes[i] = codes
+                kmat_scales[i] = scales
+            some = slice(first, first + count)
+            nc.vector.quantize_mx(
+                out=kmat_codes[i][:, some, :].rearrange("p g n -> p (g n)").bitcast(FP8X4),
+                scales=kmat_scales[i][:, some, :].rearrange("p g n -> p (g n)"),
+                in_=kmat_tiles[i][:, some, :, :].rearrange("p g n t -> p (g n t)"),
+            )
+
+        def multiply(i, h, g):
             cols = slice(h * BANK, (h + 1) * BANK)
-            out_bank = psum.tile([P, BANK], F32, tag="out_%d" % h)
-            out_banks[(i, h)] = out_bank
-            for g in range(PASSES):
-                nc.tensor.matmul_mx(
-                    out=out_bank[:],
-                    lhsT=kmat_codes[i][:, g, :].bitcast(FP8X4),
-                    lhsT_scale=kmat_scales[i][:, g, :],
-                    rhs=w_codes[:, g, cols].bitcast(FP8X4),
-                    rhs_scale=w_scales[:, g, cols],
-                    start=(g == 0),
-                    stop=(g == PASSES - 1),
-                )
+            if g == 0:
+                out_bank = psum.tile([P, BANK], F32, tag="out_%d" % h)
+                out_banks[(i, h)] = out_bank
+            nc.tensor.matmul_mx(
+                out=out_banks[(i, h)][:],
+                lhsT=kmat_codes[i][:, g, :].bitcast(FP8X4),
+                lhsT_scale=kmat_scales[i][:, g, :],
+                rhs=w_codes[:, g, cols].bitcast(FP8X4),
+                rhs_scale=w_scales[:, g, cols],
+                start=(g == 0),
+                stop=(g == PASSES - 1),
+            )
+
+        def multiply_all(i):
+            for h in range(OUT_BANKS):
+                for g in range(PASSES):
+                    multiply(i, h, g)
+
+        def empty_bank(i, h, copy):
+            if h == 0:
+                result = work.tile([P, N_OUT], F32, bufs=3)
+                results[i] = result
+            copy(out=results[i][:, h * BANK : (h + 1) * BANK], in_=out_banks[(i, h)][:])
 
         def store(i):
-            result = work.tile([P, N_OUT], F32, bufs=3)
-            nc.scalar.copy(out=result[:, :BANK], in_=out_banks[(i, 0)][:])
-            nc.scalar.copy(out=result[:, BANK:], in_=out_banks[(i, 1)][:])
-            nc.sync.dma_start(out=out_rows[:, i, :], in_=result[:])
+            for h in range(OUT_BANKS):
+                empty_bank(i, h, nc.scalar.copy)
+            nc.sync.dma_start(out=out_rows[:, i, :], in_=results[i][:])
 
         for d in range(SCALAR_DIMS + EARLY, D):
             repeat_z(d)
@@ -304,21 +319,61 @@ def tile_tmk_kernel(tc, x, design_points, chol_inv_words, chol_inv_scales, out):
         def live(i):
             return 0 <= i < ROW_TILES
 
-        for s in range(1, ROW_TILES + 5):
-            if live(s - 5):
-                store(s - 5)
+        for s in range(1, ROW_TILES):
             if live(s - 4):
-                for h in range(OUT_BANKS):
-                    multiply(s - 4, h)
-            if live(s - 1):
-                for half in range(2):
-                    add_up_transposed(s - 1, half)
+                store(s - 4)
             if live(s - 3):
-                quantise(s - 3)
+                multiply_all(s - 3)
+            open_banks(s - 1)
+            for t in range(PACK):
+                add_up_transposed(s - 1, [(g, t) for g in range(PASSES)], all_slots(s - 1))
             if live(s - 2):
-                exponentiate(s - 2)
-            if live(s):
-                new_dist(s)
-                vector_distances(s)
-                for d in range(SCALAR_DIMS):
-                    scalar_distance(s, d)
+                for g in range(PASSES):
+                    exponentiate(s - 2, g)
+            new_dist(s)
+            vector_distances(s)
+            for d in range(SCALAR_DIMS):
+                scalar_distance(s, d)
+            if live(s - 2):
+                quantise(s - 2, 0, PASSES)
+
+        last = ROW_TILES - 1
+        multiply_all(last - 2)
+        for g in range(PASSES):
+            exponentiate(last - 1, g)
+        late = slice(K_PASS, M_POINTS)
+        dist = dist_tiles[last]
+        slots = all_slots(last)
+        pairs = list(zip(slots[1::2], slots[0::2]))
+        kept = [slot for slot, other in pairs] + slots[2 * len(pairs) :]
+        for slot, other in pairs:
+            nc.vector.tensor_tensor(
+                out=dist[:, slot, late],
+                in0=dist[:, slot, late],
+                in1=z_part[:, late] if other < 0 else dist[:, other, late],
+                op=ALU.add,
+            )
+        open_banks(last)
+        for t in range(PACK):
+            add_up_transposed(last, [(0, t)], all_slots(last))
+        store(last - 3)
+        quantise(last - 1, 0, PASSES)
+        multiply_all(last - 1)
+        store(last - 2)
+        exponentiate(last, 0)
+        quantise(last, 0, 1)
+        for t in range(PACK):
+            add_up_transposed(last, [(1, t)], kept)
+        for h in range(OUT_BANKS):
+            multiply(last, h, 0)
+        empty_bank(last - 1, 0, nc.scalar.copy)
+        empty_bank(last - 1, 1, nc.vector.tensor_copy)
+        nc.sync.dma_start(out=out_rows[:, last - 1, :], in_=results[last - 1][:])
+        exponentiate(last, 1)
+        quantise(last, 1, 1)
+        for h in range(OUT_BANKS):
+            multiply(last, h, 1)
+        for h, copy, queue in ((0, nc.scalar.copy, nc.sync), (1, nc.vector.tensor_copy, nc.scalar)):
+            empty_bank(last, h, copy)
+            cols = slice(h * BANK, (h + 1) * BANK)
+            queue.dma_start(out=out_rows[:, last, cols], in_=results[last][:, cols])

@@ -30,9 +30,9 @@ OUT_BANKS = N_OUT // BANK
 
 SCALAR_DIMS = 6
 VECTOR_DIMS = D - SCALAR_DIMS
-CHAIN_COUNTS = (4, 5)
-MAX_CHAINS = max(CHAIN_COUNTS)
-SLOTS = MAX_CHAINS + SCALAR_DIMS
+CHAINS = 4
+SPLIT_T = 2
+SLOTS = CHAINS + 1 + SCALAR_DIMS
 
 EARLY = 2
 
@@ -153,20 +153,16 @@ def tile_tmk_kernel(tc, x, design_points, chol_inv_words, chol_inv_scales, out):
                 op0=ALU.mult,
                 op1=ALU.mult,
             )
-        x_parts = {}
-        for chains in CHAIN_COUNTS:
-            extra = VECTOR_DIMS % chains
-            x_part = const.tile([P, ROW_TILES, chains], F32, tag="x_part_%d" % chains)
-            x_parts[chains] = x_part
-            nc.vector.reduce_sum(
-                out=x_part[:],
-                in_=neg_x[:, :, SCALAR_DIMS : D - extra].rearrange("p i (k c) -> p i c k", c=chains),
-                axis=AX.X,
-            )
-            if extra:
-                nc.vector.tensor_tensor(
-                    out=x_part[:, :, :extra], in0=x_part[:, :, :extra], in1=neg_x[:, :, D - extra :], op=ALU.add
-                )
+        extra = VECTOR_DIMS % CHAINS
+        x_part = const.tile([P, ROW_TILES, CHAINS], F32)
+        nc.vector.reduce_sum(
+            out=x_part[:],
+            in_=neg_x[:, :, SCALAR_DIMS : D - extra].rearrange("p i (k c) -> p i c k", c=CHAINS),
+            axis=AX.X,
+        )
+        nc.vector.tensor_tensor(
+            out=x_part[:, :, :extra], in0=x_part[:, :, :extra], in1=neg_x[:, :, D - extra :], op=ALU.add
+        )
 
         out_rows = out.rearrange("(p i) c -> p i c", i=ROW_TILES)
         dist_tiles = {}
@@ -181,20 +177,19 @@ def tile_tmk_kernel(tc, x, design_points, chol_inv_words, chol_inv_scales, out):
             dist = work.tile([P, SLOTS, M_POINTS], F32, bufs=3)
             dist_tiles[i] = dist
 
-        def chains_of(i):
-            return CHAIN_COUNTS[i % len(CHAIN_COUNTS)]
+        def by_bank(columns):
+            return columns.rearrange("p (g c) -> p g c", g=PASSES)
 
         def vector_distances(i):
             dist = dist_tiles[i]
-            chains = chains_of(i)
-            for d in range(SCALAR_DIMS, D):
-                c = (d - SCALAR_DIMS) % chains
-                if d < SCALAR_DIMS + chains:
+            for d in range(SCALAR_DIMS, D - 1):
+                c = (d - SCALAR_DIMS) % CHAINS
+                if d < SCALAR_DIMS + CHAINS:
                     nc.vector.tensor_scalar(
                         out=dist[:, c, :],
                         in0=z_rep[:, d, :],
                         scalar1=two_x[:, i, d : d + 1],
-                        scalar2=x_parts[chains][:, i, c : c + 1],
+                        scalar2=x_part[:, i, c : c + 1],
                         op0=ALU.max,
                         op1=ALU.add,
                     )
@@ -207,10 +202,26 @@ def tile_tmk_kernel(tc, x, design_points, chol_inv_words, chol_inv_scales, out):
                         op0=ALU.max,
                         op1=ALU.add,
                     )
+            d = D - 1
+            c = (d - SCALAR_DIMS) % CHAINS
+            cut = SPLIT_T * P
+            nc.vector.tensor_scalar_max(
+                out=by_bank(dist[:, CHAINS, :])[:, :, :cut],
+                in0=by_bank(z_rep[:, d, :])[:, :, :cut],
+                scalar1=two_x[:, i, d : d + 1],
+            )
+            nc.vector.scalar_tensor_tensor(
+                out=by_bank(dist[:, c, :])[:, :, cut:],
+                in0=by_bank(z_rep[:, d, :])[:, :, cut:],
+                scalar=two_x[:, i, d : d + 1],
+                in1=by_bank(dist[:, c, :])[:, :, cut:],
+                op0=ALU.max,
+                op1=ALU.add,
+            )
 
         def scalar_distance(i, d):
             nc.scalar.activation(
-                out=dist_tiles[i][:, MAX_CHAINS + d, :],
+                out=dist_tiles[i][:, CHAINS + 1 + d, :],
                 in_=z_rep[:, d, :],
                 func=ACT.Abs,
                 bias=neg_x[:, i, d : d + 1],
@@ -236,8 +247,8 @@ def tile_tmk_kernel(tc, x, design_points, chol_inv_words, chol_inv_scales, out):
                         stop=(slot == slots[-1]),
                     )
 
-        def all_slots(i):
-            return [-1] + list(range(chains_of(i))) + list(range(MAX_CHAINS, SLOTS))
+        def all_slots(t):
+            return [-1] + list(range(CHAINS + 1 if t < SPLIT_T else CHAINS)) + list(range(CHAINS + 1, SLOTS))
 
         def exponentiate(i, g):
             if g == 0:
@@ -326,7 +337,7 @@ def tile_tmk_kernel(tc, x, design_points, chol_inv_words, chol_inv_scales, out):
                 multiply_all(s - 3)
             open_banks(s - 1)
             for t in range(PACK):
-                add_up_transposed(s - 1, [(g, t) for g in range(PASSES)], all_slots(s - 1))
+                add_up_transposed(s - 1, [(g, t) for g in range(PASSES)], all_slots(t))
             if live(s - 2):
                 for g in range(PASSES):
                     exponentiate(s - 2, g)
@@ -343,21 +354,29 @@ def tile_tmk_kernel(tc, x, design_points, chol_inv_words, chol_inv_scales, out):
             exponentiate(last - 1, g)
         late = slice(K_PASS, M_POINTS)
         dist = dist_tiles[last]
-        slots = all_slots(last)
-        pairs = list(zip(slots[1::2], slots[0::2]))
-        kept = [slot for slot, other in pairs] + slots[2 * len(pairs) :]
-        for slot, other in pairs:
-            nc.vector.tensor_tensor(
-                out=dist[:, slot, late],
-                in0=dist[:, slot, late],
-                in1=z_part[:, late] if other < 0 else dist[:, other, late],
-                op=ALU.add,
-            )
+
+        def add_in_pairs(slots):
+            pairs = list(zip(slots[1::2], slots[0::2]))
+            for slot, other in pairs:
+                nc.vector.tensor_tensor(
+                    out=dist[:, slot, late],
+                    in0=dist[:, slot, late],
+                    in1=z_part[:, late] if other < 0 else dist[:, other, late],
+                    op=ALU.add,
+                )
+            return [slot for slot, other in pairs] + slots[2 * len(pairs) :]
+
+        partial = slice(K_PASS, K_PASS + SPLIT_T * P)
+        nc.vector.tensor_tensor(
+            out=dist[:, 0, partial], in0=dist[:, 0, partial], in1=dist[:, CHAINS, partial], op=ALU.add
+        )
+        kept = add_in_pairs(all_slots(PACK - 1))
         open_banks(last)
         for t in range(PACK):
-            add_up_transposed(last, [(0, t)], all_slots(last))
+            add_up_transposed(last, [(0, t)], all_slots(t))
         store(last - 3)
         quantise(last - 1, 0, PASSES)
+        kept = add_in_pairs(kept)
         multiply_all(last - 1)
         store(last - 2)
         exponentiate(last, 0)

@@ -29,12 +29,11 @@ BANK = 512
 OUT_BANKS = N_OUT // BANK
 
 SCALAR_DIMS = 6
-VECTOR_DIMS = D - SCALAR_DIMS
-CHAINS = 4
-SPLIT_T = 2
-SLOTS = CHAINS + 1 + SCALAR_DIMS
-
-EARLY = 2
+OPEN_DIMS = 6
+LINK_DIMS = D - SCALAR_DIMS - OPEN_DIMS
+FIRST_OPEN = SCALAR_DIMS
+FIRST_LINK = SCALAR_DIMS + OPEN_DIMS
+COPIED = FIRST_LINK
 
 FLOPS = 2 * N_ROWS * M_POINTS * N_OUT
 
@@ -45,7 +44,7 @@ def tile_tmk_kernel(tc, x, design_points, chol_inv_words, chol_inv_scales, out):
         stack.enter_context(tc.manual_schedule())
         const = stack.enter_context(tc.tile_pool(name="const", bufs=1))
         work = stack.enter_context(tc.tile_pool(name="work", bufs=2))
-        psum = stack.enter_context(tc.psum_pool(name="psum", bufs=2))
+        psum = stack.enter_context(tc.psum_pool(name="psum", bufs=1))
 
         z_rows = const.tile([P, PASSES, PACK, D], BF16)
         nc.sync.dma_start(
@@ -54,7 +53,6 @@ def tile_tmk_kernel(tc, x, design_points, chol_inv_words, chol_inv_scales, out):
         )
         x_bf = const.tile([P, ROW_TILES, D], BF16)
         nc.scalar.dma_start(out=x_bf[:], in_=x.rearrange("(p i) d -> p i d", i=ROW_TILES))
-
         w_scales = const.tile([P, PASSES, N_OUT], U8, align_bytes=64)
         nc.vector.memset(w_scales[:].bitcast(I32), 0)
         for quadrant in range(4):
@@ -86,16 +84,14 @@ def tile_tmk_kernel(tc, x, design_points, chol_inv_words, chol_inv_scales, out):
             out=z_sum[:], in_=z_rows[:, :, :, SCALAR_DIMS:].rearrange("p g t d -> p (g t) d"), axis=AX.X
         )
         neg_z_sum = const.tile([P, BLOCKS], F32)
-        nc.vector.tensor_scalar_mul(out=neg_z_sum[:], in0=z_sum[:], scalar1=-1.0)
-        nc.vector.tensor_scalar_mul(
-            out=z_rows[:, :, :, SCALAR_DIMS:], in0=z_rows[:, :, :, SCALAR_DIMS:], scalar1=2.0
-        )
+        nc.vector.tensor_scalar_mul(out=neg_z_sum[:], in0=z_sum[:], scalar1=-0.5)
 
-        z_rep = const.tile([P, D, M_POINTS], BF16)
+        z_rep = const.tile([P, COPIED, M_POINTS], BF16)
         bank_tags = ["l1_0", "l1_1", "out_0", "out_1"]
+        z_banks = {}
 
-        def repeat_z(d):
-            z_bank = psum.tile([P, M_POINTS], BF16, tag=bank_tags[d % len(bank_tags)])
+        def repeat_z(d, tag):
+            z_bank = psum.tile([P, M_POINTS], BF16, tag=tag)
             for b in range(BLOCKS):
                 nc.tensor.matmul(
                     out=z_bank[:, b * P : (b + 1) * P],
@@ -104,10 +100,20 @@ def tile_tmk_kernel(tc, x, design_points, chol_inv_words, chol_inv_scales, out):
                     start=True,
                     stop=True,
                 )
-            nc.scalar.copy(out=z_rep[:, d, :], in_=z_bank[:])
+            z_banks[d] = z_bank
 
-        for d in range(SCALAR_DIMS, SCALAR_DIMS + EARLY):
-            repeat_z(d)
+        def keep_z(d, copy):
+            copy(out=z_rep[:, d, :], in_=z_banks[d][:])
+
+        turn = [0]
+
+        def copied_z(d, copy):
+            repeat_z(d, bank_tags[turn[0] % len(bank_tags)])
+            turn[0] += 1
+            keep_z(d, copy)
+
+        for d in range(FIRST_OPEN, FIRST_OPEN + 2):
+            copied_z(d, nc.scalar.copy)
 
         row_sum = const.tile([P, ROW_TILES], F32)
         nc.vector.reduce_sum(out=row_sum[:], in_=x_bf[:], axis=AX.X)
@@ -142,9 +148,9 @@ def tile_tmk_kernel(tc, x, design_points, chol_inv_words, chol_inv_scales, out):
         )
         rstd = const.tile([P, ROW_TILES], F32)
         nc.vector.tensor_tensor(out=rstd[:], in0=rstd_rough[:], in1=correction[:], op=ALU.mult)
-        neg_x = const.tile([P, ROW_TILES, D], F32)
-        two_x = const.tile([P, ROW_TILES, D], F32)
-        for scaled, factor in ((neg_x, -1.0 / D), (two_x, 2.0 / D)):
+        xn = const.tile([P, ROW_TILES, D], F32)
+        half_x = const.tile([P, ROW_TILES, D], F32)
+        for scaled, factor in ((xn, 1.0 / D), (half_x, -0.5 / D)):
             nc.vector.scalar_tensor_tensor(
                 out=scaled[:],
                 in0=centred[:],
@@ -153,19 +159,12 @@ def tile_tmk_kernel(tc, x, design_points, chol_inv_words, chol_inv_scales, out):
                 op0=ALU.mult,
                 op1=ALU.mult,
             )
-        extra = VECTOR_DIMS % CHAINS
-        x_part = const.tile([P, ROW_TILES, CHAINS], F32)
-        nc.vector.reduce_sum(
-            out=x_part[:],
-            in_=neg_x[:, :, SCALAR_DIMS : D - extra].rearrange("p i (k c) -> p i c k", c=CHAINS),
-            axis=AX.X,
-        )
-        nc.vector.tensor_tensor(
-            out=x_part[:, :, :extra], in0=x_part[:, :, :extra], in1=neg_x[:, :, D - extra :], op=ALU.add
-        )
+        x_part = const.tile([P, ROW_TILES], F32)
+        nc.vector.reduce_sum(out=x_part[:], in_=half_x[:, :, SCALAR_DIMS:], axis=AX.X)
 
         out_rows = out.rearrange("(p i) c -> p i c", i=ROW_TILES)
-        dist_tiles = {}
+        v_tiles = {}
+        s_tiles = {}
         l1_banks = {}
         kmat_tiles = {}
         kmat_codes = {}
@@ -174,81 +173,83 @@ def tile_tmk_kernel(tc, x, design_points, chol_inv_words, chol_inv_scales, out):
         results = {}
 
         def new_dist(i):
-            dist = work.tile([P, SLOTS, M_POINTS], F32, bufs=3)
-            dist_tiles[i] = dist
+            v_dist = work.tile([P, OPEN_DIMS, M_POINTS], F32, bufs=3)
+            s_dist = work.tile([P, SCALAR_DIMS, M_POINTS], F32, bufs=3)
+            v_tiles[i] = v_dist
+            s_tiles[i] = s_dist
 
-        def by_bank(columns):
-            return columns.rearrange("p (g c) -> p g c", g=PASSES)
+        def open_sum(i, c):
+            d = FIRST_OPEN + c
+            if c == 0:
+                nc.vector.tensor_scalar(
+                    out=v_tiles[i][:, c, :],
+                    in0=z_rep[:, d, :],
+                    scalar1=xn[:, i, d : d + 1],
+                    scalar2=x_part[:, i : i + 1],
+                    op0=ALU.max,
+                    op1=ALU.add,
+                )
+            else:
+                nc.vector.tensor_scalar_max(
+                    out=v_tiles[i][:, c, :], in0=z_rep[:, d, :], scalar1=xn[:, i, d : d + 1]
+                )
 
-        def vector_distances(i):
-            dist = dist_tiles[i]
-            for d in range(SCALAR_DIMS, D - 1):
-                c = (d - SCALAR_DIMS) % CHAINS
-                if d < SCALAR_DIMS + CHAINS:
-                    nc.vector.tensor_scalar(
-                        out=dist[:, c, :],
-                        in0=z_rep[:, d, :],
-                        scalar1=two_x[:, i, d : d + 1],
-                        scalar2=x_part[:, i, c : c + 1],
-                        op0=ALU.max,
-                        op1=ALU.add,
-                    )
-                else:
-                    nc.vector.scalar_tensor_tensor(
-                        out=dist[:, c, :],
-                        in0=z_rep[:, d, :],
-                        scalar=two_x[:, i, d : d + 1],
-                        in1=dist[:, c, :],
-                        op0=ALU.max,
-                        op1=ALU.add,
-                    )
-            d = D - 1
-            c = (d - SCALAR_DIMS) % CHAINS
-            cut = SPLIT_T * P
-            nc.vector.tensor_scalar_max(
-                out=by_bank(dist[:, CHAINS, :])[:, :, :cut],
-                in0=by_bank(z_rep[:, d, :])[:, :, :cut],
-                scalar1=two_x[:, i, d : d + 1],
-            )
+        def link(i, c):
+            d = FIRST_LINK + c
             nc.vector.scalar_tensor_tensor(
-                out=by_bank(dist[:, c, :])[:, :, cut:],
-                in0=by_bank(z_rep[:, d, :])[:, :, cut:],
-                scalar=two_x[:, i, d : d + 1],
-                in1=by_bank(dist[:, c, :])[:, :, cut:],
+                out=v_tiles[i][:, c, :],
+                in0=z_banks[d][:],
+                scalar=xn[:, i, d : d + 1],
+                in1=v_tiles[i][:, c, :],
                 op0=ALU.max,
                 op1=ALU.add,
             )
 
         def scalar_distance(i, d):
             nc.scalar.activation(
-                out=dist_tiles[i][:, CHAINS + 1 + d, :],
+                out=s_tiles[i][:, d, :],
                 in_=z_rep[:, d, :],
                 func=ACT.Abs,
-                bias=neg_x[:, i, d : d + 1],
-                scale=1.0,
+                bias=half_x[:, i, d : d + 1],
+                scale=0.5,
             )
 
-        def open_banks(i):
-            for g in range(PASSES):
-                l1_bank = psum.tile([P, PACK, P], F32, tag="l1_%d" % g)
-                l1_banks[(i, g)] = l1_bank
+        def pool_add(out_ap, in0, in1):
+            nc.gpsimd.tensor_tensor(out=out_ap, in0=in0, in1=in1, op=ALU.add)
 
-        def add_up_transposed(i, blocks, slots):
-            dist = dist_tiles[i]
-            for slot in slots:
-                for g, t in blocks:
-                    cols = slice((g * PACK + t) * P, (g * PACK + t + 1) * P)
+        def pool_adds(i):
+            v, s = v_tiles[i], s_tiles[i]
+            pool_add(v[:, 4, :], v[:, 4, :], v[:, 5, :])
+            pool_add(s[:, 0, :], s[:, 0, :], s[:, 1, :])
+
+        def columns(slot, cols):
+            kind, i, k = slot
+            if kind == "z":
+                return z_part[:, cols]
+            return (v_tiles if kind == "v" else s_tiles)[i][:, k, cols]
+
+        def slots_of(i):
+            return (
+                [("z", i, 0)]
+                + [("v", i, c) for c in range(4)]
+                + [("s", i, d) for d in range(2, SCALAR_DIMS)]
+                + [("v", i, 4), ("s", i, 0)]
+            )
+
+        def add_up_bank(i, g, slots):
+            l1_bank = psum.tile([P, PACK, P], F32, tag="l1_%d" % g)
+            l1_banks[(i, g)] = l1_bank
+            for t in range(PACK):
+                cols = slice((g * PACK + t) * P, (g * PACK + t + 1) * P)
+                for k, slot in enumerate(slots):
                     nc.tensor.matmul(
-                        out=l1_banks[(i, g)][:, t, :],
-                        lhsT=z_part[:, cols] if slot < 0 else dist[:, slot, cols],
+                        out=l1_bank[:, t, :],
+                        lhsT=columns(slot, cols),
                         rhs=ident_f32[:],
                         is_transpose=True,
-                        start=(slot == slots[0]),
-                        stop=(slot == slots[-1]),
+                        start=(k == 0),
+                        stop=(k == len(slots) - 1),
                     )
-
-        def all_slots(t):
-            return [-1] + list(range(CHAINS + 1 if t < SPLIT_T else CHAINS)) + list(range(CHAINS + 1, SLOTS))
 
         def exponentiate(i, g):
             if g == 0:
@@ -258,7 +259,7 @@ def tile_tmk_kernel(tc, x, design_points, chol_inv_words, chol_inv_scales, out):
                 out=kmat_tiles[i][:, g, :, :],
                 in_=l1_banks[(i, g)][:].rearrange("p t n -> p n t"),
                 func=ACT.Exp,
-                scale=-1.0,
+                scale=-2.0,
             )
 
         def quantise(i, first, count):
@@ -295,21 +296,24 @@ def tile_tmk_kernel(tc, x, design_points, chol_inv_words, chol_inv_scales, out):
                     multiply(i, h, g)
 
         def empty_bank(i, h, copy):
-            if h == 0:
+            if i not in results:
                 result = work.tile([P, N_OUT], F32, bufs=3)
                 results[i] = result
             copy(out=results[i][:, h * BANK : (h + 1) * BANK], in_=out_banks[(i, h)][:])
 
         def store(i):
-            for h in range(OUT_BANKS):
-                empty_bank(i, h, nc.scalar.copy)
             nc.sync.dma_start(out=out_rows[:, i, :], in_=results[i][:])
 
-        for d in range(SCALAR_DIMS + EARLY, D):
-            repeat_z(d)
+        def live(i):
+            return 0 <= i < ROW_TILES
+
+        for d in range(FIRST_OPEN + 2, FIRST_LINK):
+            copied_z(d, nc.scalar.copy)
+        for d in range(FIRST_LINK, D):
+            repeat_z(d, "z_%d" % (d - FIRST_LINK))
         z_part = const.tile([P, M_POINTS], F32)
         for g in range(PASSES):
-            part_bank = psum.tile([P, PACK, P], F32, tag=bank_tags[g])
+            part_bank = psum.tile([P, PACK, P], F32, tag=bank_tags[(turn[0] + g) % 4])
             for t in range(PACK):
                 b = g * PACK + t
                 nc.tensor.transpose(
@@ -319,80 +323,51 @@ def tile_tmk_kernel(tc, x, design_points, chol_inv_words, chol_inv_scales, out):
                 out=z_part[:, g * K_PASS : (g + 1) * K_PASS],
                 in_=part_bank[:].rearrange("p t n -> p (t n)"),
             )
+        turn[0] += 2
         new_dist(0)
-        vector_distances(0)
-        repeat_z(0)
+        for c in range(OPEN_DIMS):
+            open_sum(0, c)
+        for c in range(LINK_DIMS):
+            link(0, c)
         for d in range(SCALAR_DIMS):
-            if d + 1 < SCALAR_DIMS:
-                repeat_z(d + 1)
-            scalar_distance(0, d)
+            copied_z(d, nc.scalar.copy)
+            if d:
+                scalar_distance(0, d - 1)
+        scalar_distance(0, SCALAR_DIMS - 1)
+        pool_adds(0)
 
-        def live(i):
-            return 0 <= i < ROW_TILES
-
-        for s in range(1, ROW_TILES):
-            if live(s - 4):
-                store(s - 4)
-            if live(s - 3):
-                multiply_all(s - 3)
-            open_banks(s - 1)
-            for t in range(PACK):
-                add_up_transposed(s - 1, [(g, t) for g in range(PASSES)], all_slots(t))
+        for s in range(1, ROW_TILES + 3):
             if live(s - 2):
-                for g in range(PASSES):
-                    exponentiate(s - 2, g)
-            new_dist(s)
-            vector_distances(s)
-            for d in range(SCALAR_DIMS):
-                scalar_distance(s, d)
+                exponentiate(s - 2, 1)
+            if live(s - 3):
+                empty_bank(s - 3, 0, nc.scalar.copy)
+            if live(s):
+                new_dist(s)
+                for d in range(3):
+                    scalar_distance(s, d)
+            if live(s):
+                for c in range(3):
+                    open_sum(s, c)
             if live(s - 2):
                 quantise(s - 2, 0, PASSES)
-
-        last = ROW_TILES - 1
-        multiply_all(last - 2)
-        for g in range(PASSES):
-            exponentiate(last - 1, g)
-        late = slice(K_PASS, M_POINTS)
-        dist = dist_tiles[last]
-
-        def add_in_pairs(slots):
-            pairs = list(zip(slots[1::2], slots[0::2]))
-            for slot, other in pairs:
-                nc.vector.tensor_tensor(
-                    out=dist[:, slot, late],
-                    in0=dist[:, slot, late],
-                    in1=z_part[:, late] if other < 0 else dist[:, other, late],
-                    op=ALU.add,
-                )
-            return [slot for slot, other in pairs] + slots[2 * len(pairs) :]
-
-        partial = slice(K_PASS, K_PASS + SPLIT_T * P)
-        nc.vector.tensor_tensor(
-            out=dist[:, 0, partial], in0=dist[:, 0, partial], in1=dist[:, CHAINS, partial], op=ALU.add
-        )
-        kept = add_in_pairs(all_slots(PACK - 1))
-        open_banks(last)
-        for t in range(PACK):
-            add_up_transposed(last, [(0, t)], all_slots(t))
-        store(last - 3)
-        quantise(last - 1, 0, PASSES)
-        kept = add_in_pairs(kept)
-        multiply_all(last - 1)
-        store(last - 2)
-        exponentiate(last, 0)
-        quantise(last, 0, 1)
-        for t in range(PACK):
-            add_up_transposed(last, [(1, t)], kept)
-        for h in range(OUT_BANKS):
-            multiply(last, h, 0)
-        empty_bank(last - 1, 0, nc.scalar.copy)
-        empty_bank(last - 1, 1, nc.vector.tensor_copy)
-        nc.sync.dma_start(out=out_rows[:, last - 1, :], in_=results[last - 1][:])
-        exponentiate(last, 1)
-        quantise(last, 1, 1)
-        for h in range(OUT_BANKS):
-            multiply(last, h, 1)
-        for h, copy, queue in ((0, nc.scalar.copy, nc.sync), (1, nc.vector.tensor_copy, nc.scalar)):
-            empty_bank(last, h, copy)
-            cols = slice(h * BANK, (h + 1) * BANK)
-            queue.dma_start(out=out_rows[:, last, cols], in_=results[last][:, cols])
+            if live(s):
+                for c in range(3, OPEN_DIMS):
+                    open_sum(s, c)
+            if live(s - 3):
+                empty_bank(s - 3, 1, nc.vector.tensor_copy)
+                store(s - 3)
+            if live(s):
+                for c in range(LINK_DIMS):
+                    link(s, c)
+            if live(s - 1):
+                add_up_bank(s - 1, 0, slots_of(s - 1))
+                exponentiate(s - 1, 0)
+            if live(s):
+                for d in range(3, SCALAR_DIMS):
+                    scalar_distance(s, d)
+            if live(s - 1):
+                add_up_bank(s - 1, 1, slots_of(s - 1))
+            if live(s - 2):
+                multiply_all(s - 2)
+            if live(s):
+                pool_adds(s)

@@ -236,20 +236,22 @@ def tile_tmk_kernel(tc, x, design_points, chol_inv_words, chol_inv_scales, out):
                 + [("v", i, 4), ("s", i, 0)]
             )
 
-        def add_up_bank(i, g, slots):
-            l1_bank = psum.tile([P, PACK, P], F32, tag="l1_%d" % g)
-            l1_banks[(i, g)] = l1_bank
+        def add_up(i, slots):
+            for g in range(PASSES):
+                l1_bank = psum.tile([P, PACK, P], F32, tag="l1_%d" % g)
+                l1_banks[(i, g)] = l1_bank
             for t in range(PACK):
-                cols = slice((g * PACK + t) * P, (g * PACK + t + 1) * P)
                 for k, slot in enumerate(slots):
-                    nc.tensor.matmul(
-                        out=l1_bank[:, t, :],
-                        lhsT=columns(slot, cols),
-                        rhs=ident_f32[:],
-                        is_transpose=True,
-                        start=(k == 0),
-                        stop=(k == len(slots) - 1),
-                    )
+                    for g in range(PASSES):
+                        cols = slice((g * PACK + t) * P, (g * PACK + t + 1) * P)
+                        nc.tensor.matmul(
+                            out=l1_banks[(i, g)][:, t, :],
+                            lhsT=columns(slot, cols),
+                            rhs=ident_f32[:],
+                            is_transpose=True,
+                            start=(k == 0),
+                            stop=(k == len(slots) - 1),
+                        )
 
         def exponentiate(i, g):
             if g == 0:
@@ -337,13 +339,11 @@ def tile_tmk_kernel(tc, x, design_points, chol_inv_words, chol_inv_scales, out):
         pool_adds(0)
 
         for s in range(1, ROW_TILES + 3):
-            if live(s - 2):
-                exponentiate(s - 2, 1)
             if live(s - 3):
                 empty_bank(s - 3, 0, nc.scalar.copy)
             if live(s):
                 new_dist(s)
-                for d in range(3):
+                for d in range(SCALAR_DIMS):
                     scalar_distance(s, d)
             if live(s):
                 for c in range(3):
@@ -359,15 +359,10 @@ def tile_tmk_kernel(tc, x, design_points, chol_inv_words, chol_inv_scales, out):
             if live(s):
                 for c in range(LINK_DIMS):
                     link(s, c)
+                pool_adds(s)
             if live(s - 1):
-                add_up_bank(s - 1, 0, slots_of(s - 1))
-                exponentiate(s - 1, 0)
-            if live(s):
-                for d in range(3, SCALAR_DIMS):
-                    scalar_distance(s, d)
-            if live(s - 1):
-                add_up_bank(s - 1, 1, slots_of(s - 1))
+                add_up(s - 1, slots_of(s - 1))
+                for g in range(PASSES):
+                    exponentiate(s - 1, g)
             if live(s - 2):
                 multiply_all(s - 2)
-            if live(s):
-                pool_adds(s)

@@ -34,6 +34,10 @@ LINK_DIMS = D - SCALAR_DIMS - OPEN_DIMS
 FIRST_OPEN = SCALAR_DIMS
 FIRST_LINK = SCALAR_DIMS + OPEN_DIMS
 COPIED = FIRST_LINK
+SPLIT_T = 1
+LAST_OPEN = OPEN_DIMS - 1
+OPEN_ORDER = [4,0,1,2,3,5]
+HEAD_TILES = 6
 
 FLOPS = 2 * N_ROWS * M_POINTS * N_OUT
 
@@ -46,13 +50,22 @@ def tile_tmk_kernel(tc, x, design_points, chol_inv_words, chol_inv_scales, out):
         work = stack.enter_context(tc.tile_pool(name="work", bufs=2))
         psum = stack.enter_context(tc.psum_pool(name="psum", bufs=1))
 
+        x_bf = const.tile([P, ROW_TILES, D], BF16)
+        nc.scalar.dma_start(out=x_bf[:], in_=x.rearrange("(p i) d -> p i d", i=ROW_TILES))
         z_rows = const.tile([P, PASSES, PACK, D], BF16)
         nc.sync.dma_start(
             out=z_rows[:],
             in_=design_points.rearrange("(g p t) d -> p g t d", g=PASSES, p=P, t=PACK),
         )
-        x_bf = const.tile([P, ROW_TILES, D], BF16)
-        nc.scalar.dma_start(out=x_bf[:], in_=x.rearrange("(p i) d -> p i d", i=ROW_TILES))
+        ident_bf = const.tile([P, P], BF16)
+        make_identity(nc, ident_bf[:])
+        ident_f32 = const.tile([P, P], F32)
+        make_identity(nc, ident_f32[:])
+
+        one = const.tile([P, 1], F32)
+        nc.vector.memset(one[:], 1.0)
+        warm = const.tile([P, 1], F32)
+        nc.scalar.activation(out=warm[:], in_=one[:], func=ACT.Sqrt)
         w_scales = const.tile([P, PASSES, N_OUT], U8, align_bytes=64)
         nc.vector.memset(w_scales[:].bitcast(I32), 0)
         for quadrant in range(4):
@@ -69,26 +82,10 @@ def tile_tmk_kernel(tc, x, design_points, chol_inv_words, chol_inv_scales, out):
                 in_=chol_inv_words[g].rearrange("p n t -> p (n t)").bitcast(I32),
             )
 
-        ident_bf = const.tile([P, P], BF16)
-        make_identity(nc, ident_bf[:])
-        ident_f32 = const.tile([P, P], F32)
-        make_identity(nc, ident_f32[:])
-
-        one = const.tile([P, 1], F32)
-        nc.vector.memset(one[:], 1.0)
-        warm = const.tile([P, 1], F32)
-        nc.scalar.activation(out=warm[:], in_=one[:], func=ACT.Sqrt)
-
-        z_sum = const.tile([P, BLOCKS], F32)
-        nc.vector.reduce_sum(
-            out=z_sum[:], in_=z_rows[:, :, :, SCALAR_DIMS:].rearrange("p g t d -> p (g t) d"), axis=AX.X
-        )
-        neg_z_sum = const.tile([P, BLOCKS], F32)
-        nc.vector.tensor_scalar_mul(out=neg_z_sum[:], in0=z_sum[:], scalar1=-0.5)
-
         z_rep = const.tile([P, COPIED, M_POINTS], BF16)
-        bank_tags = ["l1_0", "l1_1", "out_0", "out_1"]
+        bank_tags = ["pair_0_0", "pair_0_1", "pair_1_0", "pair_1_1"]
         z_banks = {}
+        turn = [0]
 
         def repeat_z(d, tag):
             z_bank = psum.tile([P, M_POINTS], BF16, tag=tag)
@@ -102,65 +99,110 @@ def tile_tmk_kernel(tc, x, design_points, chol_inv_words, chol_inv_scales, out):
                 )
             z_banks[d] = z_bank
 
-        def keep_z(d, copy):
-            copy(out=z_rep[:, d, :], in_=z_banks[d][:])
-
-        turn = [0]
-
         def copied_z(d, copy):
             repeat_z(d, bank_tags[turn[0] % len(bank_tags)])
             turn[0] += 1
-            keep_z(d, copy)
-
-        for d in range(FIRST_OPEN, FIRST_OPEN + 2):
-            copied_z(d, nc.scalar.copy)
+            copy(out=z_rep[:, d, :], in_=z_banks[d][:])
 
         row_sum = const.tile([P, ROW_TILES], F32)
-        nc.vector.reduce_sum(out=row_sum[:], in_=x_bf[:], axis=AX.X)
         centred = const.tile([P, ROW_TILES, D], F32)
-        nc.vector.scalar_tensor_tensor(
-            out=centred[:],
-            in0=x_bf[:],
-            scalar=float(D),
-            in1=row_sum[:].unsqueeze(2).to_broadcast([P, ROW_TILES, D]),
-            op0=ALU.mult,
-            op1=ALU.subtract,
-        )
         squares = const.tile([P, ROW_TILES, D], F32)
-        nc.vector.tensor_tensor(out=squares[:], in0=centred[:], in1=centred[:], op=ALU.mult)
         square_sum = const.tile([P, ROW_TILES], F32)
-        nc.vector.reduce_sum(out=square_sum[:], in_=squares[:], axis=AX.X)
         var_eps = const.tile([P, ROW_TILES], F32)
-        nc.vector.tensor_scalar(
-            out=var_eps[:], in0=square_sum[:], scalar1=1.0 / D**3, scalar2=LN_EPS, op0=ALU.mult, op1=ALU.add
-        )
         std = const.tile([P, ROW_TILES], F32)
-        nc.scalar.activation(out=std[:], in_=var_eps[:], func=ACT.Sqrt)
         rstd_rough = const.tile([P, ROW_TILES], F32)
-        nc.vector.reciprocal(out=rstd_rough[:], in_=std[:])
-        y_squared = const.tile([P, ROW_TILES], F32)
-        nc.vector.tensor_tensor(out=y_squared[:], in0=rstd_rough[:], in1=rstd_rough[:], op=ALU.mult)
-        v_y_squared = const.tile([P, ROW_TILES], F32)
-        nc.vector.tensor_tensor(out=v_y_squared[:], in0=y_squared[:], in1=var_eps[:], op=ALU.mult)
+        half_y_squared = const.tile([P, ROW_TILES], F32)
         correction = const.tile([P, ROW_TILES], F32)
-        nc.vector.tensor_scalar(
-            out=correction[:], in0=v_y_squared[:], scalar1=-0.5, scalar2=1.5, op0=ALU.mult, op1=ALU.add
-        )
         rstd = const.tile([P, ROW_TILES], F32)
-        nc.vector.tensor_tensor(out=rstd[:], in0=rstd_rough[:], in1=correction[:], op=ALU.mult)
         xn = const.tile([P, ROW_TILES, D], F32)
         half_x = const.tile([P, ROW_TILES, D], F32)
-        for scaled, factor in ((xn, 1.0 / D), (half_x, -0.5 / D)):
-            nc.vector.scalar_tensor_tensor(
-                out=scaled[:],
-                in0=centred[:],
-                scalar=factor,
-                in1=rstd[:].unsqueeze(2).to_broadcast([P, ROW_TILES, D]),
-                op0=ALU.mult,
-                op1=ALU.mult,
-            )
         x_part = const.tile([P, ROW_TILES], F32)
-        nc.vector.reduce_sum(out=x_part[:], in_=half_x[:, :, SCALAR_DIMS:], axis=AX.X)
+
+        chores = []
+
+        def chore():
+            if chores:
+                step = chores[0]
+                chores.remove(step)
+                step()
+
+        def run(tiles, steps):
+            if tiles.start:
+                chores.extend(steps)
+            else:
+                for step in steps:
+                    step()
+                    chore()
+
+        def centre(tiles):
+            count = tiles.stop - tiles.start
+            run(
+                tiles,
+                [
+                    lambda: nc.vector.reduce_sum(out=row_sum[:, tiles], in_=x_bf[:, tiles, :], axis=AX.X),
+                    lambda: nc.vector.scalar_tensor_tensor(
+                        out=centred[:, tiles, :],
+                        in0=x_bf[:, tiles, :],
+                        scalar=float(D),
+                        in1=row_sum[:, tiles].unsqueeze(2).to_broadcast([P, count, D]),
+                        op0=ALU.mult,
+                        op1=ALU.subtract,
+                    ),
+                    lambda: nc.vector.tensor_tensor(
+                        out=squares[:, tiles, :], in0=centred[:, tiles, :], in1=centred[:, tiles, :], op=ALU.mult
+                    ),
+                    lambda: nc.vector.reduce_sum(out=square_sum[:, tiles], in_=squares[:, tiles, :], axis=AX.X),
+                    lambda: nc.vector.tensor_scalar(
+                        out=var_eps[:, tiles],
+                        in0=square_sum[:, tiles],
+                        scalar1=1.0 / D**3,
+                        scalar2=LN_EPS,
+                        op0=ALU.mult,
+                        op1=ALU.add,
+                    ),
+                ],
+            )
+
+        def root(tiles):
+            nc.scalar.activation(out=std[:, tiles], in_=var_eps[:, tiles], func=ACT.Sqrt)
+
+        def normalise(tiles):
+            count = tiles.stop - tiles.start
+            y = rstd_rough[:, tiles]
+
+            def scaled(which, factor):
+                nc.vector.scalar_tensor_tensor(
+                    out=which[:, tiles, :],
+                    in0=centred[:, tiles, :],
+                    scalar=factor,
+                    in1=rstd[:, tiles].unsqueeze(2).to_broadcast([P, count, D]),
+                    op0=ALU.mult,
+                    op1=ALU.mult,
+                )
+
+            run(
+                tiles,
+                [
+                    lambda: nc.vector.reciprocal(out=y, in_=std[:, tiles]),
+                    lambda: nc.vector.scalar_tensor_tensor(
+                        out=half_y_squared[:, tiles], in0=y, scalar=-0.5, in1=y, op0=ALU.mult, op1=ALU.mult
+                    ),
+                    lambda: nc.vector.tensor_tensor(
+                        out=correction[:, tiles], in0=half_y_squared[:, tiles], in1=var_eps[:, tiles], op=ALU.mult
+                    ),
+                    lambda: nc.vector.scalar_tensor_tensor(
+                        out=rstd[:, tiles], in0=correction[:, tiles], scalar=1.5, in1=y, op0=ALU.add, op1=ALU.mult
+                    ),
+                    lambda: scaled(xn, 1.0 / D),
+                    lambda: scaled(half_x, -0.5 / D),
+                ],
+            )
+
+        def sum_x(tiles):
+            run(
+                tiles,
+                [lambda: nc.vector.reduce_sum(out=x_part[:, tiles], in_=half_x[:, tiles, SCALAR_DIMS:], axis=AX.X)],
+            )
 
         out_rows = out.rearrange("(p i) c -> p i c", i=ROW_TILES)
         v_tiles = {}
@@ -172,18 +214,48 @@ def tile_tmk_kernel(tc, x, design_points, chol_inv_words, chol_inv_scales, out):
         out_banks = {}
         results = {}
 
+        def span(columns, ts):
+            if ts == ALL:
+                return columns
+            return columns.rearrange("p (g c) -> p g c", g=PASSES)[:, :, ts.start * P : ts.stop * P]
+
+        ALL = slice(0, PACK)
+        LOW = slice(0, PACK // 2)
+        HIGH = slice(PACK // 2, PACK)
+
+        def overlap(a, b):
+            first, last = max(a.start, b.start), min(a.stop, b.stop)
+            return slice(first, last) if first < last else None
+
         def new_dist(i):
             v_dist = work.tile([P, OPEN_DIMS, M_POINTS], F32, bufs=3)
             s_dist = work.tile([P, SCALAR_DIMS, M_POINTS], F32, bufs=3)
             v_tiles[i] = v_dist
             s_tiles[i] = s_dist
 
-        def open_sum(i, c):
+        def link_from(i, c, d, z, ts):
+            nc.vector.scalar_tensor_tensor(
+                out=span(v_tiles[i][:, c, :], ts),
+                in0=span(z, ts),
+                scalar=xn[:, i, d : d + 1],
+                in1=span(v_tiles[i][:, c, :], ts),
+                op0=ALU.max,
+                op1=ALU.add,
+            )
+
+        def open_sum(i, c, ts):
             d = FIRST_OPEN + c
-            if c == 0:
+            if c == LAST_OPEN:
+                linked = overlap(ts, slice(0, SPLIT_T))
+                if linked:
+                    link_from(i, c - 1, d, z_rep[:, d, :], linked)
+                ts = overlap(ts, slice(SPLIT_T, PACK))
+                if not ts:
+                    return
+            if c == 1:
                 nc.vector.tensor_scalar(
-                    out=v_tiles[i][:, c, :],
-                    in0=z_rep[:, d, :],
+                    out=span(v_tiles[i][:, c, :], ts),
+                    in0=span(z_rep[:, d, :], ts),
                     scalar1=xn[:, i, d : d + 1],
                     scalar2=x_part[:, i : i + 1],
                     op0=ALU.max,
@@ -191,62 +263,71 @@ def tile_tmk_kernel(tc, x, design_points, chol_inv_words, chol_inv_scales, out):
                 )
             else:
                 nc.vector.tensor_scalar_max(
-                    out=v_tiles[i][:, c, :], in0=z_rep[:, d, :], scalar1=xn[:, i, d : d + 1]
+                    out=span(v_tiles[i][:, c, :], ts),
+                    in0=span(z_rep[:, d, :], ts),
+                    scalar1=xn[:, i, d : d + 1],
                 )
 
-        def link(i, c):
-            d = FIRST_LINK + c
-            nc.vector.scalar_tensor_tensor(
-                out=v_tiles[i][:, c, :],
-                in0=z_banks[d][:],
-                scalar=xn[:, i, d : d + 1],
-                in1=v_tiles[i][:, c, :],
-                op0=ALU.max,
-                op1=ALU.add,
-            )
+        def link(i, c, ts):
+            link_from(i, c, FIRST_LINK + c, z_banks[FIRST_LINK + c][:], ts)
 
-        def scalar_distance(i, d):
+        def scalar_distance(i, d, ts):
             nc.scalar.activation(
-                out=s_tiles[i][:, d, :],
-                in_=z_rep[:, d, :],
+                out=span(s_tiles[i][:, d, :], ts),
+                in_=span(z_rep[:, d, :], ts),
                 func=ACT.Abs,
                 bias=half_x[:, i, d : d + 1],
                 scale=0.5,
             )
 
-        def pool_add(out_ap, in0, in1):
-            nc.gpsimd.tensor_tensor(out=out_ap, in0=in0, in1=in1, op=ALU.add)
-
-        def pool_adds(i):
-            v, s = v_tiles[i], s_tiles[i]
-            pool_add(v[:, 4, :], v[:, 4, :], v[:, 5, :])
-            pool_add(s[:, 0, :], s[:, 0, :], s[:, 1, :])
-
-        def columns(slot, cols):
-            kind, i, k = slot
-            if kind == "z":
-                return z_part[:, cols]
-            return (v_tiles if kind == "v" else s_tiles)[i][:, k, cols]
-
-        def slots_of(i):
-            return (
-                [("z", i, 0)]
-                + [("v", i, c) for c in range(4)]
-                + [("s", i, d) for d in range(2, SCALAR_DIMS)]
-                + [("v", i, 4), ("s", i, 0)]
+        def pool_add(tile, k, ts):
+            nc.gpsimd.tensor_tensor(
+                out=span(tile[:, k, :], ts), in0=span(tile[:, k, :], ts), in1=span(tile[:, k + 1, :], ts), op=ALU.add
             )
 
-        def add_up(i, slots):
-            for g in range(PASSES):
-                l1_bank = psum.tile([P, PACK, P], F32, tag="l1_%d" % g)
-                l1_banks[(i, g)] = l1_bank
-            for t in range(PACK):
-                for k, slot in enumerate(slots):
+        def pool_adds(i, ts):
+            opened = overlap(ts, slice(SPLIT_T, PACK))
+            if opened:
+                pool_add(v_tiles[i], LAST_OPEN - 1, opened)
+            pool_add(s_tiles[i], 0, ts)
+            linked = overlap(ts, slice(0, SPLIT_T))
+            if linked:
+                pool_add(s_tiles[i], 2, linked)
+
+        def slot(i, name, cols):
+            if name == "z":
+                return z_part[:, cols]
+            return (v_tiles if name[0] == "v" else s_tiles)[i][:, int(name[1]), cols]
+
+        def slots_of(t):
+            if t < SPLIT_T:
+                return ["v0", "v1", "v2", "v3", "z", "s4", "s5", "v4", "s0", "s2"]
+            return ["v0", "v1", "v2", "v3", "z", "s2", "s3", "s4", "s5", "v4", "s0"]
+
+        def open_pair(kind, tags):
+            banks = []
+            for tag in tags:
+                if kind == "l1":
+                    bank = psum.tile([P, PACK, P], F32, tag=tag)
+                else:
+                    bank = psum.tile([P, BANK], F32, tag=tag)
+                banks.append(bank)
+            return banks
+
+        def pair_tags(i):
+            return ["pair_%d_%d" % (i % 2, g) for g in range(PASSES)]
+
+        def add_up(i, ts, slots_at):
+            if ts.start == 0:
+                l1_banks[i] = open_pair("l1", pair_tags(i))
+            for t in range(ts.start, ts.stop):
+                slots = slots_at(t)
+                for k, name in enumerate(slots):
                     for g in range(PASSES):
                         cols = slice((g * PACK + t) * P, (g * PACK + t + 1) * P)
                         nc.tensor.matmul(
-                            out=l1_banks[(i, g)][:, t, :],
-                            lhsT=columns(slot, cols),
+                            out=l1_banks[i][g][:, t, :],
+                            lhsT=slot(i, name, cols),
                             rhs=ident_f32[:],
                             is_transpose=True,
                             start=(k == 0),
@@ -259,7 +340,7 @@ def tile_tmk_kernel(tc, x, design_points, chol_inv_words, chol_inv_scales, out):
                 kmat_tiles[i] = kmat
             nc.scalar.activation(
                 out=kmat_tiles[i][:, g, :, :],
-                in_=l1_banks[(i, g)][:].rearrange("p t n -> p n t"),
+                in_=l1_banks[i][g][:].rearrange("p t n -> p n t"),
                 func=ACT.Exp,
                 scale=-2.0,
             )
@@ -279,11 +360,8 @@ def tile_tmk_kernel(tc, x, design_points, chol_inv_words, chol_inv_scales, out):
 
         def multiply(i, h, g):
             cols = slice(h * BANK, (h + 1) * BANK)
-            if g == 0:
-                out_bank = psum.tile([P, BANK], F32, tag="out_%d" % h)
-                out_banks[(i, h)] = out_bank
             nc.tensor.matmul_mx(
-                out=out_banks[(i, h)][:],
+                out=out_banks[i][h][:],
                 lhsT=kmat_codes[i][:, g, :].bitcast(FP8X4),
                 lhsT_scale=kmat_scales[i][:, g, :],
                 rhs=w_codes[:, g, cols].bitcast(FP8X4),
@@ -293,6 +371,7 @@ def tile_tmk_kernel(tc, x, design_points, chol_inv_words, chol_inv_scales, out):
             )
 
         def multiply_all(i):
+            out_banks[i] = open_pair("out", pair_tags(i))
             for h in range(OUT_BANKS):
                 for g in range(PASSES):
                     multiply(i, h, g)
@@ -301,21 +380,46 @@ def tile_tmk_kernel(tc, x, design_points, chol_inv_words, chol_inv_scales, out):
             if i not in results:
                 result = work.tile([P, N_OUT], F32, bufs=3)
                 results[i] = result
-            copy(out=results[i][:, h * BANK : (h + 1) * BANK], in_=out_banks[(i, h)][:])
+            copy(out=results[i][:, h * BANK : (h + 1) * BANK], in_=out_banks[i][h][:])
 
         def store(i):
             nc.sync.dma_start(out=out_rows[:, i, :], in_=results[i][:])
 
-        def live(i):
-            return 0 <= i < ROW_TILES
-
-        for d in range(FIRST_OPEN + 2, FIRST_LINK):
-            copied_z(d, nc.scalar.copy)
-        for d in range(FIRST_LINK, D):
-            repeat_z(d, "z_%d" % (d - FIRST_LINK))
+        HEAD = slice(0, HEAD_TILES)
+        REST = slice(HEAD_TILES, ROW_TILES)
+        z_sum = const.tile([P, BLOCKS], F32)
+        neg_z_sum = const.tile([P, BLOCKS], F32)
         z_part = const.tile([P, M_POINTS], F32)
+        chores.append(
+            lambda: nc.vector.reduce_sum(
+                out=z_sum[:], in_=z_rows[:, :, :, SCALAR_DIMS:].rearrange("p g t d -> p (g t) d"), axis=AX.X
+            )
+        )
+        chores.append(lambda: nc.vector.tensor_scalar_mul(out=neg_z_sum[:], in0=z_sum[:], scalar1=-0.5))
+        copied_z(6, nc.scalar.copy)
+        centre(HEAD)
+        copied_z(7, nc.scalar.copy)
+        root(HEAD)
+        normalise(HEAD)
+        sum_x(HEAD)
+        copied_z(8, nc.scalar.copy)
+        copied_z(9, nc.scalar.copy)
+        new_dist(0)
+        open_sum(0, 0, LOW)
+        open_sum(0, 1, LOW)
+        copied_z(10, nc.scalar.copy)
+        copied_z(11, nc.scalar.copy)
+        for c in (2, 4, 3, 5):
+            open_sum(0, c, LOW)
+        copied_z(0, nc.scalar.copy)
+        copied_z(1, nc.scalar.copy)
+        copied_z(2, nc.scalar.copy)
+        copied_z(3, nc.vector.tensor_copy)
+        copied_z(4, nc.vector.tensor_copy)
+        copied_z(5, nc.vector.tensor_copy)
         for g in range(PASSES):
-            part_bank = psum.tile([P, PACK, P], F32, tag=bank_tags[(turn[0] + g) % 4])
+            part_bank = psum.tile([P, PACK, P], F32, tag=bank_tags[turn[0] % 4])
+            turn[0] += 1
             for t in range(PACK):
                 b = g * PACK + t
                 nc.tensor.transpose(
@@ -325,44 +429,121 @@ def tile_tmk_kernel(tc, x, design_points, chol_inv_words, chol_inv_scales, out):
                 out=z_part[:, g * K_PASS : (g + 1) * K_PASS],
                 in_=part_bank[:].rearrange("p t n -> p (t n)"),
             )
-        turn[0] += 2
-        new_dist(0)
-        for c in range(OPEN_DIMS):
-            open_sum(0, c)
+        centre(REST)
         for c in range(LINK_DIMS):
-            link(0, c)
-        for d in range(SCALAR_DIMS):
-            copied_z(d, nc.scalar.copy)
-            if d:
-                scalar_distance(0, d - 1)
-        scalar_distance(0, SCALAR_DIMS - 1)
-        pool_adds(0)
+            repeat_z(FIRST_LINK + c, "z_%d" % c)
+            chore()
+            link(0, c, LOW)
+        for half in (LOW, HIGH):
+            for d in range(SCALAR_DIMS):
+                scalar_distance(0, d, half)
+        for c in OPEN_ORDER:
+            open_sum(0, c, HIGH)
+            chore()
+        for c in range(LINK_DIMS):
+            link(0, c, HIGH)
 
-        for s in range(1, ROW_TILES + 3):
-            if live(s - 3):
-                empty_bank(s - 3, 0, nc.scalar.copy)
-            if live(s):
-                new_dist(s)
-                for d in range(SCALAR_DIMS):
-                    scalar_distance(s, d)
-            if live(s):
-                for c in range(3):
-                    open_sum(s, c)
+        root(REST)
+        normalise(REST)
+        sum_x(REST)
+
+        def all_slots(t):
+            return ["v0", "v1", "v2", "v3", "z", "s0", "s1", "s2", "s3", "s4", "s5", "v4"] + ["v5"] * (t >= SPLIT_T)
+
+        def live(i):
+            return 0 <= i < ROW_TILES
+
+        HALVED = [1,2]
+        for s in range(1, ROW_TILES):
             if live(s - 2):
-                quantise(s - 2, 0, PASSES)
-            if live(s):
-                for c in range(3, OPEN_DIMS):
-                    open_sum(s, c)
-            if live(s - 3):
-                empty_bank(s - 3, 1, nc.vector.tensor_copy)
-                store(s - 3)
-            if live(s):
-                for c in range(LINK_DIMS):
-                    link(s, c)
-                pool_adds(s)
-            if live(s - 1):
-                add_up(s - 1, slots_of(s - 1))
                 for g in range(PASSES):
-                    exponentiate(s - 1, g)
-            if live(s - 2):
-                multiply_all(s - 2)
+                    exponentiate(s - 2, g)
+            new_dist(s)
+            slots = slots_of if s > 1 else all_slots
+            if s in HALVED:
+                for d in range(SCALAR_DIMS):
+                    scalar_distance(s, d, LOW)
+                for c in OPEN_ORDER:
+                    open_sum(s, c, LOW)
+                    if c % 2:
+                        chore()
+                if live(s - 2):
+                    quantise(s - 2, 0, PASSES)
+                for c in range(LINK_DIMS):
+                    link(s, c, LOW)
+                pool_adds(s, LOW)
+            else:
+                for d in range(4):
+                    scalar_distance(s, d, ALL)
+                for c in OPEN_ORDER[:2]:
+                    open_sum(s, c, ALL)
+                    chore()
+                if live(s - 2):
+                    quantise(s - 2, 0, PASSES)
+                for c in OPEN_ORDER[2:]:
+                    open_sum(s, c, ALL)
+                for c in range(2):
+                    link(s, c, ALL)
+                    chore()
+            def finish(i):
+                multiply_all(i)
+                empty_bank(i, 0, nc.scalar.copy)
+                empty_bank(i, 1, nc.vector.tensor_copy if i % 2 == 0 else nc.scalar.copy)
+                store(i)
+
+            add_up(s - 1, LOW, slots)
+            if live(s - 2) and s > 1:
+                finish(s - 2)
+            add_up(s - 1, HIGH, slots)
+            if live(s - 2) and s <= 1:
+                finish(s - 2)
+            if s in HALVED:
+                for d in range(SCALAR_DIMS):
+                    scalar_distance(s, d, HIGH)
+                for c in OPEN_ORDER:
+                    open_sum(s, c, HIGH)
+                for c in range(LINK_DIMS):
+                    link(s, c, HIGH)
+                pool_adds(s, HIGH)
+            else:
+                for c in range(2, LINK_DIMS):
+                    link(s, c, ALL)
+                    chore()
+                for d in range(4, SCALAR_DIMS):
+                    scalar_distance(s, d, ALL)
+                pool_adds(s, ALL)
+
+        last = ROW_TILES - 1
+
+        def add_in_pairs(names):
+            pairs = list(zip(names[1::2], names[0::2]))
+            for name, other in pairs:
+                nc.vector.tensor_tensor(
+                    out=span(slot(last, name, slice(0, M_POINTS)), HIGH),
+                    in0=span(slot(last, name, slice(0, M_POINTS)), HIGH),
+                    in1=span(slot(last, other, slice(0, M_POINTS)), HIGH),
+                    op=ALU.add,
+                )
+            return [name for name, other in pairs] + names[2 * len(pairs) :]
+
+        for g in range(PASSES):
+            exponentiate(last - 1, g)
+        kept = add_in_pairs(["z"] + [name for name in slots_of(PACK - 1) if name != "z"])
+        quantise(last - 1, 0, PASSES)
+        kept = add_in_pairs(kept)
+        add_up(last, LOW, slots_of)
+        multiply_all(last - 1)
+        empty_bank(last - 1, 0, nc.scalar.copy)
+        empty_bank(last - 1, 1, nc.vector.tensor_copy)
+        store(last - 1)
+        add_up(last, HIGH, lambda t: kept)
+        out_banks[last] = open_pair("out", ["z_0", "z_1"])
+        for g in range(PASSES):
+            exponentiate(last, g)
+            quantise(last, g, 1)
+            for h in range(OUT_BANKS):
+                multiply(last, h, g)
+        for h, copy, queue in ((0, nc.scalar.copy, nc.sync), (1, nc.vector.tensor_copy, nc.scalar)):
+            empty_bank(last, h, copy)
+            cols = slice(h * BANK, (h + 1) * BANK)
+            queue.dma_start(out=out_rows[:, last, cols], in_=results[last][:, cols])

@@ -34,7 +34,7 @@ LINK_DIMS = D - SCALAR_DIMS - OPEN_DIMS
 FIRST_OPEN = SCALAR_DIMS
 FIRST_LINK = SCALAR_DIMS + OPEN_DIMS
 COPIED = FIRST_LINK
-SPLIT_T = 1
+SPLIT_T = 0
 LAST_OPEN = OPEN_DIMS - 1
 OPEN_ORDER = [4,0,1,2,3,5]
 HEAD_TILES = 6
@@ -488,7 +488,7 @@ def tile_tmk_kernel(tc, x, design_points, chol_inv_words, chol_inv_scales, out):
             def finish(i):
                 multiply_all(i)
                 empty_bank(i, 0, nc.scalar.copy)
-                empty_bank(i, 1, nc.vector.tensor_copy if i % 2 == 0 else nc.scalar.copy)
+                empty_bank(i, 1, nc.vector.tensor_copy if True else nc.scalar.copy)
                 store(i)
 
             add_up(s - 1, LOW, slots)

@@ -29,14 +29,17 @@ BANK = 512
 OUT_BANKS = N_OUT // BANK
 
 SCALAR_DIMS = 6
-OPEN_DIMS = 6
-LINK_DIMS = D - SCALAR_DIMS - OPEN_DIMS
-FIRST_OPEN = SCALAR_DIMS
-FIRST_LINK = SCALAR_DIMS + OPEN_DIMS
-COPIED = FIRST_LINK
-SPLIT_T = 0
-LAST_OPEN = OPEN_DIMS - 1
-OPEN_ORDER = [4,0,1,2,3,5]
+OPENED = range(6, 11)
+SUMS = len(OPENED)
+LINK_SBUF = 11
+LINKS = range(12, 16)
+COPIED = 12
+OPEN_ORDER = [4, 0, 1, 2, 3]
+SLOTS = SUMS + SCALAR_DIMS + 1
+EXTRA = SLOTS - 1
+LINKED = 3 * PASSES * P
+S0 = SUMS
+POOL_COLUMNS = 1536
 HEAD_TILES = 6
 
 FLOPS = 2 * N_ROWS * M_POINTS * N_OUT
@@ -85,23 +88,31 @@ def tile_tmk_kernel(tc, x, design_points, chol_inv_words, chol_inv_scales, out):
         z_rep = const.tile([P, COPIED, M_POINTS], BF16)
         bank_tags = ["pair_0_0", "pair_0_1", "pair_1_0", "pair_1_1"]
         z_banks = {}
-        turn = [0]
+        used = []
+
+        def next_tag():
+            used.append(0)
+            return bank_tags[(len(used) - 1) % len(bank_tags)]
+
+        def block(t, g):
+            first = (t * PASSES + g) * P
+            return slice(first, first + P)
 
         def repeat_z(d, tag):
             z_bank = psum.tile([P, M_POINTS], BF16, tag=tag)
-            for b in range(BLOCKS):
-                nc.tensor.matmul(
-                    out=z_bank[:, b * P : (b + 1) * P],
-                    lhsT=z_rows[:, b // PACK, b % PACK, d : d + 1].to_broadcast([P, P]),
-                    rhs=ident_bf[:],
-                    start=True,
-                    stop=True,
-                )
+            for t in range(PACK):
+                for g in range(PASSES):
+                    nc.tensor.matmul(
+                        out=z_bank[:, block(t, g)],
+                        lhsT=z_rows[:, g, t, d : d + 1].to_broadcast([P, P]),
+                        rhs=ident_bf[:],
+                        start=True,
+                        stop=True,
+                    )
             z_banks[d] = z_bank
 
         def copied_z(d, copy):
-            repeat_z(d, bank_tags[turn[0] % len(bank_tags)])
-            turn[0] += 1
+            repeat_z(d, next_tag())
             copy(out=z_rep[:, d, :], in_=z_banks[d][:])
 
         row_sum = const.tile([P, ROW_TILES], F32)
@@ -117,7 +128,6 @@ def tile_tmk_kernel(tc, x, design_points, chol_inv_words, chol_inv_scales, out):
         xn = const.tile([P, ROW_TILES, D], F32)
         half_x = const.tile([P, ROW_TILES, D], F32)
         x_part = const.tile([P, ROW_TILES], F32)
-
         chores = []
 
         def chore():
@@ -195,67 +205,34 @@ def tile_tmk_kernel(tc, x, design_points, chol_inv_words, chol_inv_scales, out):
                     ),
                     lambda: scaled(xn, 1.0 / D),
                     lambda: scaled(half_x, -0.5 / D),
+                    lambda: nc.vector.reduce_sum(
+                        out=x_part[:, tiles], in_=half_x[:, tiles, SCALAR_DIMS:], axis=AX.X
+                    ),
                 ],
             )
 
-        def sum_x(tiles):
-            run(
-                tiles,
-                [lambda: nc.vector.reduce_sum(out=x_part[:, tiles], in_=half_x[:, tiles, SCALAR_DIMS:], axis=AX.X)],
-            )
-
         out_rows = out.rearrange("(p i) c -> p i c", i=ROW_TILES)
-        v_tiles = {}
-        s_tiles = {}
+        dist_tiles = {}
         l1_banks = {}
         kmat_tiles = {}
         kmat_codes = {}
         kmat_scales = {}
         out_banks = {}
         results = {}
-
-        def span(columns, ts):
-            if ts == ALL:
-                return columns
-            return columns.rearrange("p (g c) -> p g c", g=PASSES)[:, :, ts.start * P : ts.stop * P]
-
-        ALL = slice(0, PACK)
-        LOW = slice(0, PACK // 2)
-        HIGH = slice(PACK // 2, PACK)
-
-        def overlap(a, b):
-            first, last = max(a.start, b.start), min(a.stop, b.stop)
-            return slice(first, last) if first < last else None
+        ALL = slice(0, M_POINTS)
+        LOW = slice(0, M_POINTS // 2)
+        HIGH = slice(M_POINTS // 2, M_POINTS)
 
         def new_dist(i):
-            v_dist = work.tile([P, OPEN_DIMS, M_POINTS], F32, bufs=3)
-            s_dist = work.tile([P, SCALAR_DIMS, M_POINTS], F32, bufs=3)
-            v_tiles[i] = v_dist
-            s_tiles[i] = s_dist
+            dist = work.tile([P, SLOTS, M_POINTS], F32, bufs=3)
+            dist_tiles[i] = dist
 
-        def link_from(i, c, d, z, ts):
-            nc.vector.scalar_tensor_tensor(
-                out=span(v_tiles[i][:, c, :], ts),
-                in0=span(z, ts),
-                scalar=xn[:, i, d : d + 1],
-                in1=span(v_tiles[i][:, c, :], ts),
-                op0=ALU.max,
-                op1=ALU.add,
-            )
-
-        def open_sum(i, c, ts):
-            d = FIRST_OPEN + c
-            if c == LAST_OPEN:
-                linked = overlap(ts, slice(0, SPLIT_T))
-                if linked:
-                    link_from(i, c - 1, d, z_rep[:, d, :], linked)
-                ts = overlap(ts, slice(SPLIT_T, PACK))
-                if not ts:
-                    return
+        def open_sum(i, c, cols):
+            d = OPENED[c]
             if c == 1:
                 nc.vector.tensor_scalar(
-                    out=span(v_tiles[i][:, c, :], ts),
-                    in0=span(z_rep[:, d, :], ts),
+                    out=dist_tiles[i][:, c, cols],
+                    in0=z_rep[:, d, cols],
                     scalar1=xn[:, i, d : d + 1],
                     scalar2=x_part[:, i : i + 1],
                     op0=ALU.max,
@@ -263,46 +240,68 @@ def tile_tmk_kernel(tc, x, design_points, chol_inv_words, chol_inv_scales, out):
                 )
             else:
                 nc.vector.tensor_scalar_max(
-                    out=span(v_tiles[i][:, c, :], ts),
-                    in0=span(z_rep[:, d, :], ts),
-                    scalar1=xn[:, i, d : d + 1],
+                    out=dist_tiles[i][:, c, cols], in0=z_rep[:, d, cols], scalar1=xn[:, i, d : d + 1]
                 )
 
-        def link(i, c, ts):
-            link_from(i, c, FIRST_LINK + c, z_banks[FIRST_LINK + c][:], ts)
+        def link(i, c, d, z):
+            nc.vector.scalar_tensor_tensor(
+                out=c,
+                in0=z,
+                scalar=xn[:, i, d : d + 1],
+                in1=c,
+                op0=ALU.max,
+                op1=ALU.add,
+            )
 
-        def scalar_distance(i, d, ts):
+        def linked_columns(i):
+            return M_POINTS if i == ROW_TILES - 1 else LINKED
+
+        def link_sbuf(i, cols):
+            limit = linked_columns(i)
+            linked = slice(cols.start, min(cols.stop, limit))
+            own = slice(max(cols.start, limit), cols.stop)
+            if linked.start < linked.stop:
+                link(i, dist_tiles[i][:, SUMS - 1, linked], LINK_SBUF, z_rep[:, LINK_SBUF, linked])
+            if own.start < own.stop:
+                nc.vector.tensor_scalar_max(
+                    out=dist_tiles[i][:, EXTRA, own],
+                    in0=z_rep[:, LINK_SBUF, own],
+                    scalar1=xn[:, i, LINK_SBUF : LINK_SBUF + 1],
+                )
+
+        def link_psum(i, c, cols):
+            link(i, dist_tiles[i][:, c, cols], LINKS[c], z_banks[LINKS[c]][:, cols])
+
+        def scalar_distance(i, d, cols):
             nc.scalar.activation(
-                out=span(s_tiles[i][:, d, :], ts),
-                in_=span(z_rep[:, d, :], ts),
+                out=dist_tiles[i][:, S0 + d, cols],
+                in_=z_rep[:, d, cols],
                 func=ACT.Abs,
                 bias=half_x[:, i, d : d + 1],
                 scale=0.5,
             )
 
-        def pool_add(tile, k, ts):
+        def pool_adds(i):
+            flat = dist_tiles[i][:].rearrange("p k c -> p (k c)")
+            first = (SUMS - 1) * M_POINTS
+            second = (S0 + 1) * M_POINTS
             nc.gpsimd.tensor_tensor(
-                out=span(tile[:, k, :], ts), in0=span(tile[:, k, :], ts), in1=span(tile[:, k + 1, :], ts), op=ALU.add
+                out=flat[:, first : first + POOL_COLUMNS],
+                in0=flat[:, first : first + POOL_COLUMNS],
+                in1=flat[:, second : second + POOL_COLUMNS],
+                op=ALU.add,
             )
 
-        def pool_adds(i, ts):
-            opened = overlap(ts, slice(SPLIT_T, PACK))
-            if opened:
-                pool_add(v_tiles[i], LAST_OPEN - 1, opened)
-            pool_add(s_tiles[i], 0, ts)
-            linked = overlap(ts, slice(0, SPLIT_T))
-            if linked:
-                pool_add(s_tiles[i], 2, linked)
+        def column(i, k, cols):
+            return z_part[:, cols] if k < 0 else dist_tiles[i][:, k, cols]
 
-        def slot(i, name, cols):
-            if name == "z":
-                return z_part[:, cols]
-            return (v_tiles if name[0] == "v" else s_tiles)[i][:, int(name[1]), cols]
+        def every_slot(i, t):
+            return [0, 1, 2, 3, -1] + [EXTRA] * (t * PASSES * P >= linked_columns(i)) + list(range(S0, EXTRA)) + [SUMS - 1]
 
-        def slots_of(t):
-            if t < SPLIT_T:
-                return ["v0", "v1", "v2", "v3", "z", "s4", "s5", "v4", "s0", "s2"]
-            return ["v0", "v1", "v2", "v3", "z", "s2", "s3", "s4", "s5", "v4", "s0"]
+        def pooled_slots(i, t):
+            done = [S0 + 1] + [S0 + 2] * ((t + 1) * PASSES * P <= POOL_COLUMNS - M_POINTS)
+            late = [S0, SUMS - 1]
+            return [k for k in every_slot(i, t) if k not in done + late] + late
 
         def open_pair(kind, tags):
             banks = []
@@ -318,20 +317,19 @@ def tile_tmk_kernel(tc, x, design_points, chol_inv_words, chol_inv_scales, out):
             return ["pair_%d_%d" % (i % 2, g) for g in range(PASSES)]
 
         def add_up(i, ts, slots_at):
-            if ts.start == 0:
+            if 0 in ts:
                 l1_banks[i] = open_pair("l1", pair_tags(i))
-            for t in range(ts.start, ts.stop):
-                slots = slots_at(t)
-                for k, name in enumerate(slots):
+            for t in ts:
+                slots = slots_at(i, t)
+                for k in slots:
                     for g in range(PASSES):
-                        cols = slice((g * PACK + t) * P, (g * PACK + t + 1) * P)
                         nc.tensor.matmul(
                             out=l1_banks[i][g][:, t, :],
-                            lhsT=slot(i, name, cols),
+                            lhsT=column(i, k, block(t, g)),
                             rhs=ident_f32[:],
                             is_transpose=True,
-                            start=(k == 0),
-                            stop=(k == len(slots) - 1),
+                            start=(k == slots[0]),
+                            stop=(k == slots[-1]),
                         )
 
         def exponentiate(i, g):
@@ -382,7 +380,9 @@ def tile_tmk_kernel(tc, x, design_points, chol_inv_words, chol_inv_scales, out):
                 results[i] = result
             copy(out=results[i][:, h * BANK : (h + 1) * BANK], in_=out_banks[i][h][:])
 
-        def store(i):
+        def empty(i):
+            empty_bank(i, 0, nc.scalar.copy)
+            empty_bank(i, 1, nc.vector.tensor_copy if i % 3 == 0 else nc.scalar.copy)
             nc.sync.dma_start(out=out_rows[:, i, :], in_=results[i][:])
 
         HEAD = slice(0, HEAD_TILES)
@@ -401,7 +401,6 @@ def tile_tmk_kernel(tc, x, design_points, chol_inv_words, chol_inv_scales, out):
         copied_z(7, nc.scalar.copy)
         root(HEAD)
         normalise(HEAD)
-        sum_x(HEAD)
         copied_z(8, nc.scalar.copy)
         copied_z(9, nc.scalar.copy)
         new_dist(0)
@@ -409,8 +408,10 @@ def tile_tmk_kernel(tc, x, design_points, chol_inv_words, chol_inv_scales, out):
         open_sum(0, 1, LOW)
         copied_z(10, nc.scalar.copy)
         copied_z(11, nc.scalar.copy)
-        for c in (2, 4, 3, 5):
-            open_sum(0, c, LOW)
+        open_sum(0, 2, LOW)
+        open_sum(0, 4, LOW)
+        open_sum(0, 3, LOW)
+        link_sbuf(0, LOW)
         copied_z(0, nc.scalar.copy)
         copied_z(1, nc.scalar.copy)
         copied_z(2, nc.scalar.copy)
@@ -418,125 +419,106 @@ def tile_tmk_kernel(tc, x, design_points, chol_inv_words, chol_inv_scales, out):
         copied_z(4, nc.vector.tensor_copy)
         copied_z(5, nc.vector.tensor_copy)
         for g in range(PASSES):
-            part_bank = psum.tile([P, PACK, P], F32, tag=bank_tags[turn[0] % 4])
-            turn[0] += 1
+            part_bank = psum.tile([P, PACK, P], F32, tag=next_tag())
             for t in range(PACK):
                 b = g * PACK + t
                 nc.tensor.transpose(
                     out=part_bank[:, t, :], in_=neg_z_sum[:, b : b + 1].to_broadcast([P, P]), identity=ident_f32[:]
                 )
             nc.scalar.copy(
-                out=z_part[:, g * K_PASS : (g + 1) * K_PASS],
-                in_=part_bank[:].rearrange("p t n -> p (t n)"),
+                out=z_part[:].rearrange("p (t g c) -> p t g c", t=PACK, g=PASSES)[:, :, g, :],
+                in_=part_bank[:],
             )
         centre(REST)
-        for c in range(LINK_DIMS):
-            repeat_z(FIRST_LINK + c, "z_%d" % c)
+        for c, d in enumerate(LINKS):
+            repeat_z(d, "z_%d" % c)
             chore()
-            link(0, c, LOW)
+            link_psum(0, c, LOW)
         for half in (LOW, HIGH):
             for d in range(SCALAR_DIMS):
                 scalar_distance(0, d, half)
         for c in OPEN_ORDER:
             open_sum(0, c, HIGH)
             chore()
-        for c in range(LINK_DIMS):
-            link(0, c, HIGH)
-
+        link_sbuf(0, HIGH)
+        for c in range(len(LINKS)):
+            link_psum(0, c, HIGH)
         root(REST)
         normalise(REST)
-        sum_x(REST)
-
-        def all_slots(t):
-            return ["v0", "v1", "v2", "v3", "z", "s0", "s1", "s2", "s3", "s4", "s5", "v4"] + ["v5"] * (t >= SPLIT_T)
 
         def live(i):
             return 0 <= i < ROW_TILES
 
-        HALVED = [1,2]
+        HALVED = [1]
         for s in range(1, ROW_TILES):
-            if live(s - 2):
+            new_dist(s)
+            slots_at = every_slot if s - 1 in HALVED or s == 1 else pooled_slots
+            if s in HALVED:
+                if live(s - 2):
+                    for g in range(PASSES):
+                        exponentiate(s - 2, g)
+                for cols in (LOW, HIGH):
+                    for d in range(SCALAR_DIMS):
+                        scalar_distance(s, d, cols)
+                    for c in OPEN_ORDER:
+                        open_sum(s, c, cols)
+                        if c % 2:
+                            chore()
+                    if live(s - 2) and cols == LOW:
+                        quantise(s - 2, 0, PASSES)
+                    link_sbuf(s, cols)
+                    for c in range(len(LINKS)):
+                        link_psum(s, c, cols)
+                add_up(s - 1, (0, 1), slots_at)
+                if live(s - 2):
+                    multiply_all(s - 2)
+                    empty(s - 2)
+                add_up(s - 1, (2, 3), slots_at)
+            else:
+                scalar_distance(s, 0, ALL)
                 for g in range(PASSES):
                     exponentiate(s - 2, g)
-            new_dist(s)
-            slots = slots_of if s > 1 else all_slots
-            if s in HALVED:
-                for d in range(SCALAR_DIMS):
-                    scalar_distance(s, d, LOW)
-                for c in OPEN_ORDER:
-                    open_sum(s, c, LOW)
-                    if c % 2:
-                        chore()
-                if live(s - 2):
-                    quantise(s - 2, 0, PASSES)
-                for c in range(LINK_DIMS):
-                    link(s, c, LOW)
-                pool_adds(s, LOW)
-            else:
-                for d in range(4):
+                for d in range(1, 5):
                     scalar_distance(s, d, ALL)
-                for c in OPEN_ORDER[:2]:
+                for c in OPEN_ORDER:
                     open_sum(s, c, ALL)
                     chore()
-                if live(s - 2):
-                    quantise(s - 2, 0, PASSES)
-                for c in OPEN_ORDER[2:]:
-                    open_sum(s, c, ALL)
-                for c in range(2):
-                    link(s, c, ALL)
+                quantise(s - 2, 0, PASSES)
+                link_sbuf(s, ALL)
+                for c in range(len(LINKS)):
+                    link_psum(s, c, ALL)
                     chore()
-            def finish(i):
-                multiply_all(i)
-                empty_bank(i, 0, nc.scalar.copy)
-                empty_bank(i, 1, nc.vector.tensor_copy if True else nc.scalar.copy)
-                store(i)
-
-            add_up(s - 1, LOW, slots)
-            if live(s - 2) and s > 1:
-                finish(s - 2)
-            add_up(s - 1, HIGH, slots)
-            if live(s - 2) and s <= 1:
-                finish(s - 2)
-            if s in HALVED:
-                for d in range(SCALAR_DIMS):
-                    scalar_distance(s, d, HIGH)
-                for c in OPEN_ORDER:
-                    open_sum(s, c, HIGH)
-                for c in range(LINK_DIMS):
-                    link(s, c, HIGH)
-                pool_adds(s, HIGH)
-            else:
-                for c in range(2, LINK_DIMS):
-                    link(s, c, ALL)
-                    chore()
-                for d in range(4, SCALAR_DIMS):
-                    scalar_distance(s, d, ALL)
-                pool_adds(s, ALL)
+                add_up(s - 1, (0, 1), slots_at)
+                multiply_all(s - 2)
+                empty(s - 2)
+                scalar_distance(s, 5, ALL)
+                add_up(s - 1, (2, 3), slots_at)
+                pool_adds(s)
 
         last = ROW_TILES - 1
 
-        def add_in_pairs(names):
-            pairs = list(zip(names[1::2], names[0::2]))
-            for name, other in pairs:
+        def add_in_pairs(slots):
+            pairs = list(zip(slots[1::2], slots[0::2]))
+            for k, other in pairs:
                 nc.vector.tensor_tensor(
-                    out=span(slot(last, name, slice(0, M_POINTS)), HIGH),
-                    in0=span(slot(last, name, slice(0, M_POINTS)), HIGH),
-                    in1=span(slot(last, other, slice(0, M_POINTS)), HIGH),
+                    out=dist_tiles[last][:, k, HIGH],
+                    in0=dist_tiles[last][:, k, HIGH],
+                    in1=column(last, other, HIGH),
                     op=ALU.add,
                 )
-            return [name for name, other in pairs] + names[2 * len(pairs) :]
+            return [k for k, other in pairs] + slots[2 * len(pairs) :]
 
         for g in range(PASSES):
             exponentiate(last - 1, g)
-        kept = add_in_pairs(["z"] + [name for name in slots_of(PACK - 1) if name != "z"])
+        kept = add_in_pairs([-1] + [k for k in pooled_slots(last, PACK - 1) if k >= 0])
         quantise(last - 1, 0, PASSES)
         kept = add_in_pairs(kept)
-        add_up(last, LOW, slots_of)
+        add_up(last, (0, 1), pooled_slots)
         multiply_all(last - 1)
         empty_bank(last - 1, 0, nc.scalar.copy)
         empty_bank(last - 1, 1, nc.vector.tensor_copy)
-        store(last - 1)
-        add_up(last, HIGH, lambda t: kept)
+        nc.sync.dma_start(out=out_rows[:, last - 1, :], in_=results[last - 1][:])
+        add_up(last, (2, 3), lambda i, t: kept)
         out_banks[last] = open_pair("out", ["z_0", "z_1"])
         for g in range(PASSES):
             exponentiate(last, g)

@@ -40,6 +40,7 @@ EXTRA = SLOTS - 1
 LINKED = 3 * PASSES * P
 S0 = SUMS
 POOL_COLUMNS = 1536
+PLAIN_T = [1,2]
 HEAD_TILES = 6
 
 FLOPS = 2 * N_ROWS * M_POINTS * N_OUT
@@ -106,6 +107,7 @@ def tile_tmk_kernel(tc, x, design_points, chol_inv_words, chol_inv_scales, out):
                         out=z_bank[:, block(t, g)],
                         lhsT=z_rows[:, g, t, d : d + 1].to_broadcast([P, P]),
                         rhs=ident_bf[:],
+                        is_transpose=(len(z_banks) >= 9),
                         start=True,
                         stop=True,
                     )
@@ -323,11 +325,12 @@ def tile_tmk_kernel(tc, x, design_points, chol_inv_words, chol_inv_scales, out):
                 slots = slots_at(i, t)
                 for k in slots:
                     for g in range(PASSES):
+                        plain = k < 0 and t in PLAIN_T
                         nc.tensor.matmul(
                             out=l1_banks[i][g][:, t, :],
-                            lhsT=column(i, k, block(t, g)),
-                            rhs=ident_f32[:],
-                            is_transpose=True,
+                            lhsT=z_terms[:, block(t, g)] if plain else column(i, k, block(t, g)),
+                            rhs=three[:] if plain else ident_f32[:],
+                            is_transpose=not plain,
                             start=(k == slots[0]),
                             stop=(k == slots[-1]),
                         )
@@ -396,6 +399,31 @@ def tile_tmk_kernel(tc, x, design_points, chol_inv_words, chol_inv_scales, out):
             )
         )
         chores.append(lambda: nc.vector.tensor_scalar_mul(out=neg_z_sum[:], in0=z_sum[:], scalar1=-0.5))
+        pieces = const.tile([P, PACK, PASSES, P], BF16)
+        nc.gpsimd.memset(pieces[:], 0.0)
+        three = const.tile([P, P], BF16)
+        nc.gpsimd.memset(three[:], 0.0)
+        nc.gpsimd.memset(three[0:3, :], 1.0)
+        left_1 = const.tile([P, BLOCKS], F32)
+        left_2 = const.tile([P, BLOCKS], F32)
+        z_terms = const.tile([P, M_POINTS], BF16)
+
+        def piece(k):
+            return pieces[:, :, :, k].rearrange("p t g -> p g t")
+
+        def by_block(small):
+            return small[:].rearrange("p (g t) -> p g t", g=PASSES)
+
+        for step in (
+            lambda: nc.vector.tensor_copy(out=piece(0), in_=by_block(neg_z_sum)),
+            lambda: nc.vector.tensor_tensor(
+                out=by_block(left_1), in0=by_block(neg_z_sum), in1=piece(0), op=ALU.subtract
+            ),
+            lambda: nc.vector.tensor_copy(out=piece(1), in_=by_block(left_1)),
+            lambda: nc.vector.tensor_tensor(out=by_block(left_2), in0=by_block(left_1), in1=piece(1), op=ALU.subtract),
+            lambda: nc.vector.tensor_copy(out=piece(2), in_=by_block(left_2)),
+        ):
+            chores.append(step)
         copied_z(6, nc.scalar.copy)
         centre(HEAD)
         copied_z(7, nc.scalar.copy)
@@ -429,6 +457,11 @@ def tile_tmk_kernel(tc, x, design_points, chol_inv_words, chol_inv_scales, out):
                 out=z_part[:].rearrange("p (t g c) -> p t g c", t=PACK, g=PASSES)[:, :, g, :],
                 in_=part_bank[:],
             )
+        terms_bank = psum.tile([P, M_POINTS], BF16, tag=next_tag())
+        for t in range(PACK):
+            for g in range(PASSES):
+                nc.tensor.transpose(out=terms_bank[:, block(t, g)], in_=pieces[:, t, g, :], identity=ident_bf[:])
+        nc.scalar.copy(out=z_terms[:], in_=terms_bank[:])
         centre(REST)
         for c, d in enumerate(LINKS):
             repeat_z(d, "z_%d" % c)

@@ -37,7 +37,7 @@ COPIED = 12
 OPEN_ORDER = [4, 0, 1, 2, 3]
 SLOTS = SUMS + SCALAR_DIMS + 1
 EXTRA = SLOTS - 1
-LINKED = 3 * PASSES * P
+LINKED = 1 * PASSES * P
 S0 = SUMS
 POOL_COLUMNS = 1536
 PLAIN_T = [1,2]
@@ -385,7 +385,7 @@ def tile_tmk_kernel(tc, x, design_points, chol_inv_words, chol_inv_scales, out):
 
         def empty(i):
             empty_bank(i, 0, nc.scalar.copy)
-            empty_bank(i, 1, nc.vector.tensor_copy if i % 3 == 0 else nc.scalar.copy)
+            empty_bank(i, 1, nc.vector.tensor_copy if i % 4 == 0 else nc.scalar.copy)
             nc.sync.dma_start(out=out_rows[:, i, :], in_=results[i][:])
 
         HEAD = slice(0, HEAD_TILES)

@@ -371,6 +371,19 @@ def tile_tmk_kernel(tc, x, design_points, chol_inv_words, chol_inv_scales, out):
                 stop=(g == PASSES - 1),
             )
 
+        def keep_clock(count):
+            idle_bank = psum.tile([P, BANK], F32, tag="pair_1_1")
+            for k in range(count):
+                nc.tensor.matmul_mx(
+                    out=idle_bank[:],
+                    lhsT=w_codes[:, 0, :P].bitcast(FP8X4),
+                    lhsT_scale=w_scales[:, 0, :P],
+                    rhs=w_codes[:, 0, :BANK].bitcast(FP8X4),
+                    rhs_scale=w_scales[:, 0, :BANK],
+                    start=True,
+                    stop=True,
+                )
+
         def multiply_all(i):
             out_banks[i] = open_pair("out", pair_tags(i))
             for h in range(OUT_BANKS):
@@ -385,7 +398,7 @@ def tile_tmk_kernel(tc, x, design_points, chol_inv_words, chol_inv_scales, out):
 
         def empty(i):
             empty_bank(i, 0, nc.scalar.copy)
-            empty_bank(i, 1, nc.vector.tensor_copy if i % 4 == 0 else nc.scalar.copy)
+            empty_bank(i, 1, nc.vector.tensor_copy if i % 4 == 3 else nc.scalar.copy)
             nc.sync.dma_start(out=out_rows[:, i, :], in_=results[i][:])
 
         HEAD = slice(0, HEAD_TILES)
@@ -485,6 +498,8 @@ def tile_tmk_kernel(tc, x, design_points, chol_inv_words, chol_inv_scales, out):
         HALVED = [1]
         for s in range(1, ROW_TILES):
             new_dist(s)
+            if s == 1:
+                keep_clock(6)
             slots_at = every_slot if s - 1 in HALVED or s == 1 else pooled_slots
             if s in HALVED:
                 if live(s - 2):
@@ -551,7 +566,17 @@ def tile_tmk_kernel(tc, x, design_points, chol_inv_words, chol_inv_scales, out):
         empty_bank(last - 1, 0, nc.scalar.copy)
         empty_bank(last - 1, 1, nc.vector.tensor_copy)
         nc.sync.dma_start(out=out_rows[:, last - 1, :], in_=results[last - 1][:])
-        add_up(last, (2, 3), lambda i, t: kept)
+        for g in range(PASSES):
+            for t in (2, 3):
+                for k in kept:
+                    nc.tensor.matmul(
+                        out=l1_banks[last][g][:, t, :],
+                        lhsT=column(last, k, block(t, g)),
+                        rhs=ident_f32[:],
+                        is_transpose=True,
+                        start=(k == kept[0]),
+                        stop=(k == kept[-1]),
+                    )
         out_banks[last] = open_pair("out", ["z_0", "z_1"])
         for g in range(PASSES):
             exponentiate(last, g)

from contextlib import ExitStack

import concourse.mybir as mybir
from concourse.masks import make_identity

F32 = mybir.dt.float32
BF16 = mybir.dt.bfloat16
I32 = mybir.dt.int32
U32 = mybir.dt.uint32
U8 = mybir.dt.uint8
FP8X4 = mybir.dt.float8_e4m3fn_x4
ALU = mybir.AluOpType
ACT = mybir.ActivationFunctionType
AX = mybir.AxisListType

N_ROWS = 4096
M_POINTS = 1024
N_OUT = 1024
D = 16
LN_EPS = 1e-5

P = 128
PACK = 4
K_PASS = P * PACK
PASSES = M_POINTS // K_PASS
BLOCKS = PASSES * PACK
ROW_TILES = N_ROWS // P
BANK = 512
OUT_BANKS = N_OUT // BANK

SCALAR_DIMS = 6
OPENED = range(6, 11)
SUMS = len(OPENED)
LINK_SBUF = 11
LINKS = range(12, 16)
COPIED = 12
OPEN_ORDER = [4, 0, 1, 2, 3]
SLOTS = SUMS + SCALAR_DIMS + 1
EXTRA = SLOTS - 1
LINKED = 1 * PASSES * P
S0 = SUMS
POOL_COLUMNS = 1536
PLAIN_T = [1,2]
HEAD_TILES = 6

FLOPS = 2 * N_ROWS * M_POINTS * N_OUT


def tile_tmk_kernel(tc, x, design_points, chol_inv_words, chol_inv_scales, out):
    nc = tc.nc
    with ExitStack() as stack:
        stack.enter_context(tc.manual_schedule())
        const = stack.enter_context(tc.tile_pool(name="const", bufs=1))
        work = stack.enter_context(tc.tile_pool(name="work", bufs=2))
        psum = stack.enter_context(tc.psum_pool(name="psum", bufs=1))

        x_bf = const.tile([P, ROW_TILES, D], BF16)
        nc.scalar.dma_start(out=x_bf[:], in_=x.rearrange("(p i) d -> p i d", i=ROW_TILES))
        z_rows = const.tile([P, PASSES, PACK, D], BF16)
        nc.sync.dma_start(
            out=z_rows[:],
            in_=design_points.rearrange("(g p t) d -> p g t d", g=PASSES, p=P, t=PACK),
        )
        ident_bf = const.tile([P, P], BF16)
        make_identity(nc, ident_bf[:])
        ident_f32 = const.tile([P, P], F32)
        make_identity(nc, ident_f32[:])

        one = const.tile([P, 1], F32)
        nc.vector.memset(one[:], 1.0)
        warm = const.tile([P, 1], F32)
        nc.scalar.activation(out=warm[:], in_=one[:], func=ACT.Sqrt)
        w_scales = const.tile([P, PASSES, N_OUT], U8, align_bytes=64)
        nc.vector.memset(w_scales[:].bitcast(I32), 0)
        for quadrant in range(4):
            nc.sync.dma_start(
                out=w_scales[32 * quadrant : 32 * quadrant + 4, :, :].bitcast(I32),
                in_=chol_inv_scales[:, 4 * quadrant : 4 * quadrant + 4, :]
                .rearrange("g r n -> r g n")
                .bitcast(I32),
            )
        w_codes = const.tile([P, PASSES, N_OUT], U32, align_bytes=64)
        for g in range(PASSES):
            nc.sync.dma_start(
                out=w_codes[:, g, :].bitcast(I32),
                in_=chol_inv_words[g].rearrange("p n t -> p (n t)").bitcast(I32),
            )

        z_rep = const.tile([P, COPIED, M_POINTS], BF16)
        bank_tags = ["pair_0_0", "pair_0_1", "pair_1_0", "pair_1_1"]
        z_banks = {}
        used = []

        def next_tag():
            used.append(0)
            return bank_tags[(len(used) - 1) % len(bank_tags)]

        def block(t, g):
            first = (t * PASSES + g) * P
            return slice(first, first + P)

        def repeat_z(d, tag):
            z_bank = psum.tile([P, M_POINTS], BF16, tag=tag)
            for t in range(PACK):
                for g in range(PASSES):
                    nc.tensor.matmul(
                        out=z_bank[:, block(t, g)],
                        lhsT=z_rows[:, g, t, d : d + 1].to_broadcast([P, P]),
                        rhs=ident_bf[:],
                        is_transpose=(len(z_banks) >= 9),
                        start=True,
                        stop=True,
                    )
            z_banks[d] = z_bank

        def copied_z(d, copy):
            repeat_z(d, next_tag())
            copy(out=z_rep[:, d, :], in_=z_banks[d][:])

        row_sum = const.tile([P, ROW_TILES], F32)
        centred = const.tile([P, ROW_TILES, D], F32)
        squares = const.tile([P, ROW_TILES, D], F32)
        square_sum = const.tile([P, ROW_TILES], F32)
        var_eps = const.tile([P, ROW_TILES], F32)
        std = const.tile([P, ROW_TILES], F32)
        rstd_rough = const.tile([P, ROW_TILES], F32)
        half_y_squared = const.tile([P, ROW_TILES], F32)
        correction = const.tile([P, ROW_TILES], F32)
        rstd = const.tile([P, ROW_TILES], F32)
        xn = const.tile([P, ROW_TILES, D], F32)
        half_x = const.tile([P, ROW_TILES, D], F32)
        x_part = const.tile([P, ROW_TILES], F32)
        chores = []

        def chore():
            if chores:
                step = chores[0]
                chores.remove(step)
                step()

        def run(tiles, steps):
            if tiles.start:
                chores.extend(steps)
            else:
                for step in steps:
                    step()
                    chore()

        def centre(tiles):
            count = tiles.stop - tiles.start
            run(
                tiles,
                [
                    lambda: nc.vector.reduce_sum(out=row_sum[:, tiles], in_=x_bf[:, tiles, :], axis=AX.X),
                    lambda: nc.vector.scalar_tensor_tensor(
                        out=centred[:, tiles, :],
                        in0=x_bf[:, tiles, :],
                        scalar=float(D),
                        in1=row_sum[:, tiles].unsqueeze(2).to_broadcast([P, count, D]),
                        op0=ALU.mult,
                        op1=ALU.subtract,
                    ),
                    lambda: nc.vector.tensor_tensor(
                        out=squares[:, tiles, :], in0=centred[:, tiles, :], in1=centred[:, tiles, :], op=ALU.mult
                    ),
                    lambda: nc.vector.reduce_sum(out=square_sum[:, tiles], in_=squares[:, tiles, :], axis=AX.X),
                    lambda: nc.vector.tensor_scalar(
                        out=var_eps[:, tiles],
                        in0=square_sum[:, tiles],
                        scalar1=1.0 / D**3,
                        scalar2=LN_EPS,
                        op0=ALU.mult,
                        op1=ALU.add,
                    ),
                ],
            )

        def root(tiles):
            nc.scalar.activation(out=std[:, tiles], in_=var_eps[:, tiles], func=ACT.Sqrt)

        def normalise(tiles):
            count = tiles.stop - tiles.start
            y = rstd_rough[:, tiles]

            def scaled(which, factor):
                nc.vector.scalar_tensor_tensor(
                    out=which[:, tiles, :],
                    in0=centred[:, tiles, :],
                    scalar=factor,
                    in1=rstd[:, tiles].unsqueeze(2).to_broadcast([P, count, D]),
                    op0=ALU.mult,
                    op1=ALU.mult,
                )

            run(
                tiles,
                [
                    lambda: nc.vector.reciprocal(out=y, in_=std[:, tiles]),
                    lambda: nc.vector.scalar_tensor_tensor(
                        out=half_y_squared[:, tiles], in0=y, scalar=-0.5, in1=y, op0=ALU.mult, op1=ALU.mult
                    ),
                    lambda: nc.vector.tensor_tensor(
                        out=correction[:, tiles], in0=half_y_squared[:, tiles], in1=var_eps[:, tiles], op=ALU.mult
                    ),
                    lambda: nc.vector.scalar_tensor_tensor(
                        out=rstd[:, tiles], in0=correction[:, tiles], scalar=1.5, in1=y, op0=ALU.add, op1=ALU.mult
                    ),
                    lambda: scaled(xn, 1.0 / D),
                    lambda: scaled(half_x, -0.5 / D),
                    lambda: nc.vector.reduce_sum(
                        out=x_part[:, tiles], in_=half_x[:, tiles, SCALAR_DIMS:], axis=AX.X
                    ),
                ],
            )

        out_rows = out.rearrange("(p i) c -> p i c", i=ROW_TILES)
        dist_tiles = {}
        l1_banks = {}
        kmat_tiles = {}
        kmat_codes = {}
        kmat_scales = {}
        out_banks = {}
        results = {}
        ALL = slice(0, M_POINTS)
        LOW = slice(0, M_POINTS // 2)
        HIGH = slice(M_POINTS // 2, M_POINTS)

        def new_dist(i):
            dist = work.tile([P, SLOTS, M_POINTS], F32, bufs=3)
            dist_tiles[i] = dist

        def open_sum(i, c, cols):
            d = OPENED[c]
            if c == 1:
                nc.vector.tensor_scalar(
                    out=dist_tiles[i][:, c, cols],
                    in0=z_rep[:, d, cols],
                    scalar1=xn[:, i, d : d + 1],
                    scalar2=x_part[:, i : i + 1],
                    op0=ALU.max,
                    op1=ALU.add,
                )
            else:
                nc.vector.tensor_scalar_max(
                    out=dist_tiles[i][:, c, cols], in0=z_rep[:, d, cols], scalar1=xn[:, i, d : d + 1]
                )

        def link(i, c, d, z):
            nc.vector.scalar_tensor_tensor(
                out=c,
                in0=z,
                scalar=xn[:, i, d : d + 1],
                in1=c,
                op0=ALU.max,
                op1=ALU.add,
            )

        def linked_columns(i):
            return M_POINTS if i == ROW_TILES - 1 else LINKED

        def link_sbuf(i, cols):
            limit = linked_columns(i)
            linked = slice(cols.start, min(cols.stop, limit))
            own = slice(max(cols.start, limit), cols.stop)
            if linked.start < linked.stop:
                link(i, dist_tiles[i][:, SUMS - 1, linked], LINK_SBUF, z_rep[:, LINK_SBUF, linked])
            if own.start < own.stop:
                nc.vector.tensor_scalar_max(
                    out=dist_tiles[i][:, EXTRA, own],
                    in0=z_rep[:, LINK_SBUF, own],
                    scalar1=xn[:, i, LINK_SBUF : LINK_SBUF + 1],
                )

        def link_psum(i, c, cols):
            link(i, dist_tiles[i][:, c, cols], LINKS[c], z_banks[LINKS[c]][:, cols])

        def scalar_distance(i, d, cols):
            nc.scalar.activation(
                out=dist_tiles[i][:, S0 + d, cols],
                in_=z_rep[:, d, cols],
                func=ACT.Abs,
                bias=half_x[:, i, d : d + 1],
                scale=0.5,
            )

        def pool_adds(i):
            flat = dist_tiles[i][:].rearrange("p k c -> p (k c)")
            first = (SUMS - 1) * M_POINTS
            second = (S0 + 1) * M_POINTS
            nc.gpsimd.tensor_tensor(
                out=flat[:, first : first + POOL_COLUMNS],
                in0=flat[:, first : first + POOL_COLUMNS],
                in1=flat[:, second : second + POOL_COLUMNS],
                op=ALU.add,
            )

        def column(i, k, cols):
            return z_part[:, cols] if k < 0 else dist_tiles[i][:, k, cols]

        def every_slot(i, t):
            return [0, 1, 2, 3, -1] + [EXTRA] * (t * PASSES * P >= linked_columns(i)) + list(range(S0, EXTRA)) + [SUMS - 1]

        def pooled_slots(i, t):
            done = [S0 + 1] + [S0 + 2] * ((t + 1) * PASSES * P <= POOL_COLUMNS - M_POINTS)
            late = [S0, SUMS - 1]
            return [k for k in every_slot(i, t) if k not in done + late] + late

        def open_pair(kind, tags):
            banks = []
            for tag in tags:
                if kind == "l1":
                    bank = psum.tile([P, PACK, P], F32, tag=tag)
                else:
                    bank = psum.tile([P, BANK], F32, tag=tag)
                banks.append(bank)
            return banks

        def pair_tags(i):
            return ["pair_%d_%d" % (i % 2, g) for g in range(PASSES)]

        def add_up(i, ts, slots_at):
            if 0 in ts:
                l1_banks[i] = open_pair("l1", pair_tags(i))
            for t in ts:
                slots = slots_at(i, t)
                for k in slots:
                    for g in range(PASSES):
                        plain = k < 0 and t in PLAIN_T
                        nc.tensor.matmul(
                            out=l1_banks[i][g][:, t, :],
                            lhsT=z_terms[:, block(t, g)] if plain else column(i, k, block(t, g)),
                            rhs=three[:] if plain else ident_f32[:],
                            is_transpose=not plain,
                            start=(k == slots[0]),
                            stop=(k == slots[-1]),
                        )

        def exponentiate(i, g):
            if g == 0:
                kmat = work.tile([P, PASSES, P, PACK], BF16, align_bytes=64)
                kmat_tiles[i] = kmat
            nc.scalar.activation(
                out=kmat_tiles[i][:, g, :, :],
                in_=l1_banks[i][g][:].rearrange("p t n -> p n t"),
                func=ACT.Exp,
                scale=-2.0,
            )

        def quantise(i, first, count):
            if first == 0:
                codes = work.tile([P, PASSES, P], U32, align_bytes=64)
                scales = work.tile([P, PASSES, P], U8, align_bytes=64)
                kmat_codes[i] = codes
                kmat_scales[i] = scales
            some = slice(first, first + count)
            nc.vector.quantize_mx(
                out=kmat_codes[i][:, some, :].rearrange("p g n -> p (g n)").bitcast(FP8X4),
                scales=kmat_scales[i][:, some, :].rearrange("p g n -> p (g n)"),
                in_=kmat_tiles[i][:, some, :, :].rearrange("p g n t -> p (g n t)"),
            )

        def multiply(i, h, g):
            cols = slice(h * BANK, (h + 1) * BANK)
            nc.tensor.matmul_mx(
                out=out_banks[i][h][:],
                lhsT=kmat_codes[i][:, g, :].bitcast(FP8X4),
                lhsT_scale=kmat_scales[i][:, g, :],
                rhs=w_codes[:, g, cols].bitcast(FP8X4),
                rhs_scale=w_scales[:, g, cols],
                start=(g == 0),
                stop=(g == PASSES - 1),
            )

        def keep_clock(count):
            idle_bank = psum.tile([P, BANK], F32, tag="pair_1_1")
            for k in range(count):
                nc.tensor.matmul_mx(
                    out=idle_bank[:],
                    lhsT=w_codes[:, 0, :P].bitcast(FP8X4),
                    lhsT_scale=w_scales[:, 0, :P],
                    rhs=w_codes[:, 0, :BANK].bitcast(FP8X4),
                    rhs_scale=w_scales[:, 0, :BANK],
                    start=True,
                    stop=True,
                )

        def multiply_all(i):
            out_banks[i] = open_pair("out", pair_tags(i))
            for h in range(OUT_BANKS):
                for g in range(PASSES):
                    multiply(i, h, g)

        def empty_bank(i, h, copy):
            if i not in results:
                result = work.tile([P, N_OUT], F32, bufs=3)
                results[i] = result
            copy(out=results[i][:, h * BANK : (h + 1) * BANK], in_=out_banks[i][h][:])

        def empty(i):
            empty_bank(i, 0, nc.scalar.copy)
            empty_bank(i, 1, nc.vector.tensor_copy if i % 4 == 3 else nc.scalar.copy)
            nc.sync.dma_start(out=out_rows[:, i, :], in_=results[i][:])

        HEAD = slice(0, HEAD_TILES)
        REST = slice(HEAD_TILES, ROW_TILES)
        z_sum = const.tile([P, BLOCKS], F32)
        neg_z_sum = const.tile([P, BLOCKS], F32)
        z_part = const.tile([P, M_POINTS], F32)
        chores.append(
            lambda: nc.vector.reduce_sum(
                out=z_sum[:], in_=z_rows[:, :, :, SCALAR_DIMS:].rearrange("p g t d -> p (g t) d"), axis=AX.X
            )
        )
        chores.append(lambda: nc.vector.tensor_scalar_mul(out=neg_z_sum[:], in0=z_sum[:], scalar1=-0.5))
        pieces = const.tile([P, PACK, PASSES, P], BF16)
        nc.gpsimd.memset(pieces[:], 0.0)
        three = const.tile([P, P], BF16)
        nc.gpsimd.memset(three[:], 0.0)
        nc.gpsimd.memset(three[0:3, :], 1.0)
        left_1 = const.tile([P, BLOCKS], F32)
        left_2 = const.tile([P, BLOCKS], F32)
        z_terms = const.tile([P, M_POINTS], BF16)

        def piece(k):
            return pieces[:, :, :, k].rearrange("p t g -> p g t")

        def by_block(small):
            return small[:].rearrange("p (g t) -> p g t", g=PASSES)

        for step in (
            lambda: nc.vector.tensor_copy(out=piece(0), in_=by_block(neg_z_sum)),
            lambda: nc.vector.tensor_tensor(
                out=by_block(left_1), in0=by_block(neg_z_sum), in1=piece(0), op=ALU.subtract
            ),
            lambda: nc.vector.tensor_copy(out=piece(1), in_=by_block(left_1)),
            lambda: nc.vector.tensor_tensor(out=by_block(left_2), in0=by_block(left_1), in1=piece(1), op=ALU.subtract),
            lambda: nc.vector.tensor_copy(out=piece(2), in_=by_block(left_2)),
        ):
            chores.append(step)
        copied_z(6, nc.scalar.copy)
        centre(HEAD)
        copied_z(7, nc.scalar.copy)
        root(HEAD)
        normalise(HEAD)
        copied_z(8, nc.scalar.copy)
        copied_z(9, nc.scalar.copy)
        new_dist(0)
        open_sum(0, 0, LOW)
        open_sum(0, 1, LOW)
        copied_z(10, nc.scalar.copy)
        copied_z(11, nc.scalar.copy)
        open_sum(0, 2, LOW)
        open_sum(0, 4, LOW)
        open_sum(0, 3, LOW)
        link_sbuf(0, LOW)
        copied_z(0, nc.scalar.copy)
        copied_z(1, nc.scalar.copy)
        copied_z(2, nc.scalar.copy)
        copied_z(3, nc.vector.tensor_copy)
        copied_z(4, nc.vector.tensor_copy)
        copied_z(5, nc.vector.tensor_copy)
        for g in range(PASSES):
            part_bank = psum.tile([P, PACK, P], F32, tag=next_tag())
            for t in range(PACK):
                b = g * PACK + t
                nc.tensor.transpose(
                    out=part_bank[:, t, :], in_=neg_z_sum[:, b : b + 1].to_broadcast([P, P]), identity=ident_f32[:]
                )
            nc.scalar.copy(
                out=z_part[:].rearrange("p (t g c) -> p t g c", t=PACK, g=PASSES)[:, :, g, :],
                in_=part_bank[:],
            )
        terms_bank = psum.tile([P, M_POINTS], BF16, tag=next_tag())
        for t in range(PACK):
            for g in range(PASSES):
                nc.tensor.transpose(out=terms_bank[:, block(t, g)], in_=pieces[:, t, g, :], identity=ident_bf[:])
        nc.scalar.copy(out=z_terms[:], in_=terms_bank[:])
        centre(REST)
        for c, d in enumerate(LINKS):
            repeat_z(d, "z_%d" % c)
            chore()
            link_psum(0, c, LOW)
        for half in (LOW, HIGH):
            for d in range(SCALAR_DIMS):
                scalar_distance(0, d, half)
        for c in OPEN_ORDER:
            open_sum(0, c, HIGH)
            chore()
        link_sbuf(0, HIGH)
        for c in range(len(LINKS)):
            link_psum(0, c, HIGH)
        root(REST)
        normalise(REST)

        def live(i):
            return 0 <= i < ROW_TILES

        HALVED = [1]
        for s in range(1, ROW_TILES):
            new_dist(s)
            if s == 1:
                keep_clock(6)
            slots_at = every_slot if s - 1 in HALVED or s == 1 else pooled_slots
            if s in HALVED:
                if live(s - 2):
                    for g in range(PASSES):
                        exponentiate(s - 2, g)
                for cols in (LOW, HIGH):
                    for d in range(SCALAR_DIMS):
                        scalar_distance(s, d, cols)
                    for c in OPEN_ORDER:
                        open_sum(s, c, cols)
                        if c % 2:
                            chore()
                    if live(s - 2) and cols == LOW:
                        quantise(s - 2, 0, PASSES)
                    link_sbuf(s, cols)
                    for c in range(len(LINKS)):
                        link_psum(s, c, cols)
                add_up(s - 1, (0, 1), slots_at)
                if live(s - 2):
                    multiply_all(s - 2)
                    empty(s - 2)
                add_up(s - 1, (2, 3), slots_at)
            else:
                scalar_distance(s, 0, ALL)
                for g in range(PASSES):
                    exponentiate(s - 2, g)
                for d in range(1, 5):
                    scalar_distance(s, d, ALL)
                for c in OPEN_ORDER:
                    open_sum(s, c, ALL)
                    chore()
                quantise(s - 2, 0, PASSES)
                link_sbuf(s, ALL)
                for c in range(len(LINKS)):
                    link_psum(s, c, ALL)
                    chore()
                add_up(s - 1, (0, 1), slots_at)
                multiply_all(s - 2)
                empty(s - 2)
                scalar_distance(s, 5, ALL)
                add_up(s - 1, (2, 3), slots_at)
                pool_adds(s)

        last = ROW_TILES - 1

        def add_in_pairs(slots):
            pairs = list(zip(slots[1::2], slots[0::2]))
            for k, other in pairs:
                nc.vector.tensor_tensor(
                    out=dist_tiles[last][:, k, HIGH],
                    in0=dist_tiles[last][:, k, HIGH],
                    in1=column(last, other, HIGH),
                    op=ALU.add,
                )
            return [k for k, other in pairs] + slots[2 * len(pairs) :]

        for g in range(PASSES):
            exponentiate(last - 1, g)
        kept = add_in_pairs([-1] + [k for k in pooled_slots(last, PACK - 1) if k >= 0])
        quantise(last - 1, 0, PASSES)
        kept = add_in_pairs(kept)
        add_up(last, (0, 1), pooled_slots)
        multiply_all(last - 1)
        empty_bank(last - 1, 0, nc.scalar.copy)
        empty_bank(last - 1, 1, nc.vector.tensor_copy)
        nc.sync.dma_start(out=out_rows[:, last - 1, :], in_=results[last - 1][:])
        for g in range(PASSES):
            for t in (2, 3):
                for k in kept:
                    nc.tensor.matmul(
                        out=l1_banks[last][g][:, t, :],
                        lhsT=column(last, k, block(t, g)),
                        rhs=ident_f32[:],
                        is_transpose=True,
                        start=(k == kept[0]),
                        stop=(k == kept[-1]),
                    )
        out_banks[last] = open_pair("out", ["z_0", "z_1"])
        for g in range(PASSES):
            exponentiate(last, g)
            quantise(last, g, 1)
            for h in range(OUT_BANKS):
                multiply(last, h, g)
        for h, copy, queue in ((0, nc.scalar.copy, nc.sync), (1, nc.vector.tensor_copy, nc.scalar)):
            empty_bank(last, h, copy)
            cols = slice(h * BANK, (h + 1) * BANK)
            queue.dma_start(out=out_rows[:, last, cols], in_=results[last][:, cols])
